import numpy as np
import ml_dtypes


def mxq(x, axis, fmt="e4m3"):
    dtype, down = {"e4m3": (ml_dtypes.float8_e4m3fn, 7), "e5m2": (ml_dtypes.float8_e5m2, 14)}[fmt]
    v = np.moveaxis(np.asarray(x, np.float32).astype(ml_dtypes.bfloat16).astype(np.float64), axis, -1)
    blocks = v.reshape(v.shape[:-1] + (-1, 32))
    amax = np.abs(blocks).max(-1, keepdims=True)
    byte = np.maximum(np.where(amax > 0, np.frexp(amax)[1] - 1 + 127, 0) - down, 1)
    scale = np.exp2(byte - 127.0)
    codes = (blocks / scale).astype(np.float32).astype(dtype).astype(np.float64)
    return np.moveaxis((codes * scale).reshape(v.shape), -1, axis)


WIDE = False


def mx_kscale(k):
    if not WIDE:
        return np.ones(k)
    levels = np.array([10, -10, 5, -5, 0])
    if k % 512:
        return np.exp2(np.random.permutation(np.resize(levels, k // 32))).repeat(32)
    a = np.empty((k // 512, 16))
    for p in range(k // 512):
        a[p, :8] = np.random.permutation(np.resize(levels, 8))
        for g in range(8):
            far = levels[np.abs(levels - a[p, g]) >= 10]
            a[p, g + 8] = far[np.random.randint(len(far))]
    return np.exp2(a.ravel()).repeat(32)


BF16 = ml_dtypes.bfloat16


def bf(x):
    return np.asarray(x, np.float32).astype(BF16)


def f64(x):
    return np.asarray(x).astype(np.float64)


B, H, P, D, NF, DO, G = 2, 12, 32, 512, 8, 512, 5
N = D * H * P


def setup_inputs():
    s = mx_kscale(D)
    return {
        "x": bf(np.random.standard_normal((B, H, P, D)) * s),
        "lin_w": bf(np.random.standard_normal((G * D, D)) * 0.3 / np.sqrt(D) / s),
        "lin_b": bf(np.random.standard_normal(G * D) * 0.1),
        "grid": bf(np.arange(NF)[None, :] + 1.0 + 0.1 * np.random.standard_normal((G, NF))),
        "coef": bf(np.random.standard_normal((N, NF, G)) * 0.5),
        "shift": bf(np.random.standard_normal((1, H, G, P, D)) * 0.5),
    }


def reference(x, lin_w, lin_b, grid, coef, shift):
    xl = (mxq(f64(x), 3, "e4m3") @ mxq(f64(lin_w).T, 0, "e4m3")) + f64(lin_b)
    xl = xl.reshape(B, G, N)
    sn = np.sin(f64(grid)[None, :, :, None] * xl[:, :, None, :])
    f = sn * f64(coef).transpose(2, 1, 0)[None]
    return f.reshape(B, H, G, NF, P, D).sum(axis=3) + f64(shift)

@@ -1,0 +1,293 @@
+import math
+from contextlib import ExitStack
+
+import concourse.mybir as mybir
+from concourse.masks import make_identity
+
+F32 = mybir.dt.float32
+BF16 = mybir.dt.bfloat16
+I32 = mybir.dt.int32
+U32 = mybir.dt.uint32
+U8 = mybir.dt.uint8
+FP8X4 = mybir.dt.float8_e4m3fn_x4
+ALU = mybir.AluOpType
+ACT = mybir.ActivationFunctionType
+
+P = 128
+BATCH = 2
+X_ROWS = 384
+K = 512
+W_BLOCKS = 20
+GROUPS = 5
+FREQS = 8
+SEG = 128
+TILES = 12
+UNIT_TILES = 4
+UNITS = TILES // UNIT_TILES
+UNIT = UNIT_TILES * SEG
+WINDOW = 128
+WINDOW_STEP = 64
+ROWS = 78
+TERMS = 8
+WHOLE_AHEAD = 2
+PRODUCT_LAG = 2
+STORE_LAG = 2
+
+FLOPS = 2 * BATCH * X_ROWS * K * W_BLOCKS * P
+
+
+def tile_ka_attention_heads_mod_pa_kernel(tc, x, lin_w, lin_b, grid, coef, shift, out):
+    nc = tc.nc
+
+    x_view = x.rearrange("b h p k -> (b h p) k").rearrange("(a p) k -> p a k", p=P)
+    w_view = lin_w.rearrange("(a p) k -> p a k", p=P)
+    coef_view = coef.rearrange("(t q d) m j -> t q (d m j)", q=P, d=SEG)
+    shift_view = shift.rearrange("o h g p (c d) -> (p c) (o h g) d", d=SEG)
+    out_view = out.rearrange("b h g p (c d) -> (p c) b (h g) d", d=SEG)
+
+    with ExitStack() as stack:
+        keep = stack.enter_context(tc.tile_pool(name="keep", bufs=1))
+        psum_turn = stack.enter_context(tc.psum_pool(name="psum_turn", bufs=4))
+        psum_acc = stack.enter_context(tc.psum_pool(name="psum_acc", bufs=2))
+        psum_sums = stack.enter_context(tc.psum_pool(name="psum_sums", bufs=2))
+
+        x_tiles = BATCH * X_ROWS // P
+        x_codes = keep.tile([P, x_tiles * P], U32, name="x_codes", align_bytes=64)
+        x_scales = keep.tile([P, x_tiles * P], U8, name="x_scales", align_bytes=64)
+        w_codes = keep.tile([P, W_BLOCKS * P], U32, name="w_codes", align_bytes=64)
+        w_scales = keep.tile([P, W_BLOCKS * P], U8, name="w_scales", align_bytes=64)
+        coef_sb = keep.tile([P, TILES * SEG, FREQS * GROUPS], BF16, name="coef_sb")
+        ident = keep.tile([P, P], F32, name="ident")
+        ident_bf = keep.tile([P, P], BF16, name="ident_bf")
+        bias_t = keep.tile([P, W_BLOCKS], F32, name="bias_t")
+        turns = keep.tile([P, GROUPS * FREQS], F32, name="turns")
+        minus_quarter = keep.tile([P, 1], F32, name="minus_quarter")
+        quarter_turn = keep.tile([P, 1], F32, name="quarter_turn")
+
+        with tc.tile_pool(name="prep", bufs=1) as prep:
+            x_raw = prep.tile([P, x_tiles * K], BF16, name="x_raw")
+            w_raw = prep.tile([P, W_BLOCKS * K], BF16, name="w_raw")
+            x_grouped = prep.tile([P, x_tiles * P * 4], BF16, name="x_grouped", align_bytes=64)
+            w_grouped = prep.tile([P, W_BLOCKS * P * 4], BF16, name="w_grouped", align_bytes=64)
+            bias_rows = prep.tile([P, P], BF16, name="bias_rows")
+            bias_rows_f = prep.tile([P, P], F32, name="bias_rows_f")
+            grid_bc = prep.tile([P, GROUPS * FREQS], BF16, name="grid_bc")
+
+            nc.vector.memset(bias_rows[:], 0.0)
+            nc.vector.memset(minus_quarter[:], -0.25)
+            nc.vector.tensor_scalar(
+                out=quarter_turn[:], in0=minus_quarter[:], scalar1=-2.0 * math.pi, scalar2=None, op0=ALU.mult
+            )
+            make_identity(nc, ident[:])
+            make_identity(nc, ident_bf[:])
+
+            nc.sync.dma_start(out=x_raw[:].rearrange("p (a k) -> p a k", k=K), in_=x_view)
+            for c in range(GROUPS):
+                nc.sync.dma_start(
+                    out=w_raw[:, c * 4 * K : (c + 1) * 4 * K].rearrange("p (a k) -> p a k", k=K),
+                    in_=w_view[:, c * 4 : (c + 1) * 4, :],
+                )
+            for t in range(TILES):
+                nc.sync.dma_start(
+                    out=coef_sb[:, t * SEG : (t + 1) * SEG, :].rearrange("p d c -> p (d c)"),
+                    in_=coef_view[t],
+                )
+            nc.scalar.dma_start(out=bias_rows[0:W_BLOCKS, :], in_=lin_b.rearrange("(a d) -> a d", d=P))
+            nc.scalar.dma_start(out=grid_bc[:], in_=grid.rearrange("j m -> (j m)").partition_broadcast(P))
+
+            nc.vector.tensor_scalar(
+                out=turns[:], in0=grid_bc[:], scalar1=1.0 / (2.0 * math.pi), scalar2=None, op0=ALU.mult
+            )
+
+            nc.vector.tensor_copy(out=bias_rows_f[:], in_=bias_rows[:])
+            bias_ps = psum_acc.tile([P, UNIT], F32, name="bias_ps", tag="acc")
+            nc.tensor.transpose(bias_ps[:, 0:P], bias_rows_f[:], ident[:])
+            nc.vector.tensor_copy(out=bias_t[:], in_=bias_ps[:, 0:W_BLOCKS])
+
+            def put_k_on_partitions(raw, grouped, n_tiles):
+                words = raw[:].bitcast(F32)
+                grouped_words = grouped[:].bitcast(F32)
+                for pair in range(n_tiles // 2):
+                    bank = psum_turn.tile([P, UNIT], F32, name="turned", tag="bank")
+                    for a in range(2):
+                        for u in range(2):
+                            first = (pair * 2 + a) * 2 * P
+                            nc.tensor.transpose(
+                                bank[:, (a * 2 + u) * P : (a * 2 + u + 1) * P],
+                                words[:, first + u : first + 2 * P : 2],
+                                ident[:],
+                            )
+                    dst = grouped_words[:, pair * UNIT : (pair + 1) * UNIT].rearrange(
+                        "p (a r u) -> p a r u", a=2, u=2
+                    )
+                    src = bank[:].rearrange("p (a u r) -> p a r u", a=2, u=2)
+                    if pair % 2 == 0:
+                        nc.vector.tensor_copy(out=dst, in_=src)
+                    else:
+                        nc.scalar.copy(out=dst, in_=src)
+
+            def quantise(grouped, codes, scales, n_rows):
+                for first in range(0, n_rows, 512):
+                    n = min(512, n_rows - first)
+                    nc.vector.quantize_mx(
+                        out=codes[:, first : first + n].bitcast(FP8X4),
+                        scales=scales[:, first : first + n],
+                        in_=grouped[:, first * 4 : (first + n) * 4],
+                    )
+
+            put_k_on_partitions(x_raw, x_grouped, x_tiles)
+            put_k_on_partitions(w_raw, w_grouped, W_BLOCKS)
+            quantise(x_grouped, x_codes, x_scales, x_tiles * P)
+            quantise(w_grouped, w_codes, w_scales, W_BLOCKS * P)
+
+        loop = stack.enter_context(tc.tile_pool(name="loop", bufs=2))
+        halves = GROUPS * FREQS * UNITS
+        halves_per_group = FREQS * UNITS
+
+        def project(j):
+            first_row = min((2 * SEG * j) // W_BLOCKS, WINDOW - ROWS)
+            shift_sb = loop.tile([P, TILES, SEG], BF16, name="shift_sb")
+            nc.sync.dma_start(out=shift_sb[:], in_=shift_view[:, j * TILES : (j + 1) * TILES, :])
+            xl_t = loop.tile([P, BATCH, ROWS * W_BLOCKS], F32, name="xl_t")
+            for b in range(BATCH):
+                window = b * X_ROWS + WINDOW_STEP * j
+                for c in range(GROUPS):
+                    acc = psum_acc.tile([P, UNIT], F32, name="acc", tag="acc")
+                    for d in range(4):
+                        a = c * 4 + d
+                        nc.tensor.matmul_mx(
+                            out=acc[:, d * WINDOW : (d + 1) * WINDOW],
+                            lhsT=w_codes[:, a * P : (a + 1) * P].bitcast(FP8X4),
+                            lhsT_scale=w_scales[:, a * P : (a + 1) * P],
+                            rhs=x_codes[:, window : window + WINDOW].bitcast(FP8X4),
+                            rhs_scale=x_scales[:, window : window + WINDOW],
+                            start=True,
+                            stop=True,
+                        )
+                    nc.vector.tensor_tensor(
+                        out=xl_t[:, b, :].rearrange("p (r a) -> p r a", a=W_BLOCKS)[:, :, c * 4 : (c + 1) * 4],
+                        in0=acc[:].rearrange("p (d r) -> p r d", d=4)[:, first_row : first_row + ROWS, :],
+                        in1=bias_t[:, c * 4 : (c + 1) * 4].unsqueeze(1).to_broadcast([P, ROWS, 4]),
+                        op=ALU.add,
+                    )
+            return xl_t, 2 * SEG * j - W_BLOCKS * first_row, shift_sb
+
+        def turn_coef(i):
+            jm, unit = divmod(i, UNITS)
+            j, m = divmod(jm, FREQS)
+            column = m * GROUPS + j
+            turned = psum_turn.tile([P, UNIT], BF16, name="coef_ps", tag="bank")
+            for t in range(UNIT_TILES):
+                first = (unit * UNIT_TILES + t) * SEG
+                nc.tensor.transpose(
+                    turned[:, t * SEG : (t + 1) * SEG], coef_sb[:, first : first + SEG, column], ident_bf[:]
+                )
+            return turned
+
+
+        def xl_of_half(i):
+            xl_t, first_seg = xl_of[i // halves_per_group][0:2]
+            unit = i % UNITS
+            return xl_t[:, :, first_seg + unit * UNIT : first_seg + (unit + 1) * UNIT]
+
+        def whole_turns(i):
+            whole = loop.tile([P, BATCH, UNIT], I32, name="whole", bufs=WHOLE_AHEAD + 1)
+            nc.gpsimd.tensor_scalar(
+                out=whole[:],
+                in0=xl_of_half(i),
+                scalar1=turns[:, i // UNITS : i // UNITS + 1],
+                scalar2=-0.25,
+                op0=ALU.mult,
+                op1=ALU.add,
+            )
+            return whole
+
+        def rest_of_turn(i, whole):
+            rest = loop.tile([P, BATCH, UNIT], F32, name="rest", bufs=3)
+            nc.vector.scalar_tensor_tensor(
+                out=rest[:],
+                in0=xl_of_half(i),
+                scalar=turns[:, i // UNITS : i // UNITS + 1],
+                in1=whole[:],
+                op0=ALU.mult,
+                op1=ALU.subtract,
+            )
+            return rest
+
+        def distance(rest):
+            nc.scalar.activation(out=rest[:], in_=rest[:], func=ACT.Abs, bias=minus_quarter[:, 0:1])
+
+        def sine_of_distance(rest):
+            sine = loop.tile([P, BATCH, UNIT], F32, name="sine", bufs=3)
+            nc.scalar.activation(
+                out=sine[:], in_=rest[:], func=ACT.Sin, scale=-2.0 * math.pi, bias=quarter_turn[:, 0:1]
+            )
+            return sine
+
+        def four_terms(sine, coef_t):
+            products = loop.tile([P, BATCH, UNIT], F32, name="products", bufs=5)
+            nc.vector.tensor_tensor(
+                out=products[:],
+                in0=sine[:],
+                in1=coef_t[:].unsqueeze(1).to_broadcast([P, BATCH, UNIT]),
+                op=ALU.mult,
+            )
+            return products
+
+        def add_up(block):
+            sums = psum_sums.tile([P, BATCH, SEG], F32, name="sums")
+            for b in range(BATCH):
+                for e in range(TERMS):
+                    products = products_of[2 * block + e // UNIT_TILES]
+                    t = e % UNIT_TILES
+                    nc.tensor.matmul(
+                        out=sums[:, b, :],
+                        lhsT=products[:, b, t * SEG : (t + 1) * SEG],
+                        rhs=ident[:],
+                        is_transpose=True,
+                        start=(e == 0),
+                        stop=(e == TERMS - 1),
+                    )
+            sums_of[block] = sums
+
+        def store(block):
+            total = loop.tile([P, BATCH, SEG], F32, name="total")
+            nc.vector.tensor_tensor(
+                out=total[:],
+                in0=sums_of[block][:],
+                in1=xl_of[block // TILES][2][:, block % TILES : block % TILES + 1, :].to_broadcast([P, BATCH, SEG]),
+                op=ALU.add,
+            )
+            nc.sync.dma_start(out=out_view[:, :, block, :], in_=total[:])
+
+        coef_t_of = {}
+        whole_of = {}
+        rest_of = {}
+        sine_of = {}
+        products_of = {}
+        sums_of = {}
+        with tc.manual_schedule():
+            xl_of = {0: project(0)}
+            for i in range(WHOLE_AHEAD):
+                whole_of[i] = whole_turns(i)
+            for i in range(halves + PRODUCT_LAG + STORE_LAG + 1):
+                if i + WHOLE_AHEAD < halves:
+                    whole_of[i + WHOLE_AHEAD] = whole_turns(i + WHOLE_AHEAD)
+                if i < halves:
+                    rest_of[i] = rest_of_turn(i, whole_of[i])
+                if 1 <= i <= halves:
+                    sine_of[i - 1] = sine_of_distance(rest_of[i - 1])
+                if i < halves:
+                    coef_t_of[i] = turn_coef(i)
+                    distance(rest_of[i])
+                multiplied = i - PRODUCT_LAG
+                if 0 <= multiplied < halves:
+                    products_of[multiplied] = four_terms(sine_of[multiplied], coef_t_of[multiplied])
+                stored = multiplied - STORE_LAG
+                if stored >= 0 and stored % 2 == 1:
+                    store(stored // 2)
+                if 0 <= multiplied < halves and multiplied % 2 == 1:
+                    add_up(multiplied // 2)
+                j, local = divmod(i, halves_per_group)
+                if j + 1 < GROUPS and local == halves_per_group // 2:
+                    xl_of[j + 1] = project(j + 1)

@@ -61,8 +61,6 @@ def tile_ka_attention_heads_mod_pa_kernel(tc, x, lin_w, lin_b, grid, coef, shift
         ident_bf = keep.tile([P, P], BF16, name="ident_bf")
         bias_t = keep.tile([P, W_BLOCKS], F32, name="bias_t")
         turns = keep.tile([P, GROUPS * FREQS], F32, name="turns")
-        minus_quarter = keep.tile([P, 1], F32, name="minus_quarter")
-        quarter_turn = keep.tile([P, 1], F32, name="quarter_turn")
 
         with tc.tile_pool(name="prep", bufs=1) as prep:
             x_raw = prep.tile([P, x_tiles * K], BF16, name="x_raw")
@@ -74,10 +72,6 @@ def tile_ka_attention_heads_mod_pa_kernel(tc, x, lin_w, lin_b, grid, coef, shift
             grid_bc = prep.tile([P, GROUPS * FREQS], BF16, name="grid_bc")
 
             nc.vector.memset(bias_rows[:], 0.0)
-            nc.vector.memset(minus_quarter[:], -0.25)
-            nc.vector.tensor_scalar(
-                out=quarter_turn[:], in0=minus_quarter[:], scalar1=-2.0 * math.pi, scalar2=None, op0=ALU.mult
-            )
             make_identity(nc, ident[:])
             make_identity(nc, ident_bf[:])
 
@@ -196,7 +190,7 @@ def tile_ka_attention_heads_mod_pa_kernel(tc, x, lin_w, lin_b, grid, coef, shift
                 out=whole[:],
                 in0=xl_of_half(i),
                 scalar1=turns[:, i // UNITS : i // UNITS + 1],
-                scalar2=-0.25,
+                scalar2=0.0,
                 op0=ALU.mult,
                 op1=ALU.add,
             )
@@ -214,14 +208,9 @@ def tile_ka_attention_heads_mod_pa_kernel(tc, x, lin_w, lin_b, grid, coef, shift
             )
             return rest
 
-        def distance(rest):
-            nc.scalar.activation(out=rest[:], in_=rest[:], func=ACT.Abs, bias=minus_quarter[:, 0:1])
-
-        def sine_of_distance(rest):
+        def sine_of_rest(rest):
             sine = loop.tile([P, BATCH, UNIT], F32, name="sine", bufs=3)
-            nc.scalar.activation(
-                out=sine[:], in_=rest[:], func=ACT.Sin, scale=-2.0 * math.pi, bias=quarter_turn[:, 0:1]
-            )
+            nc.scalar.activation(out=sine[:], in_=rest[:], func=ACT.Sin, scale=2.0 * math.pi)
             return sine
 
         def four_terms(sine, coef_t):
@@ -276,10 +265,9 @@ def tile_ka_attention_heads_mod_pa_kernel(tc, x, lin_w, lin_b, grid, coef, shift
                 if i < halves:
                     rest_of[i] = rest_of_turn(i, whole_of[i])
                 if 1 <= i <= halves:
-                    sine_of[i - 1] = sine_of_distance(rest_of[i - 1])
+                    sine_of[i - 1] = sine_of_rest(rest_of[i - 1])
                 if i < halves:
                     coef_t_of[i] = turn_coef(i)
-                    distance(rest_of[i])
                 multiplied = i - PRODUCT_LAG
                 if 0 <= multiplied < halves:
                     products_of[multiplied] = four_terms(sine_of[multiplied], coef_t_of[multiplied])

@@ -30,8 +30,13 @@ WINDOW_STEP = 64
 ROWS = 78
 TERMS = 8
 WHOLE_AHEAD = 2
-PRODUCT_LAG = 2
-STORE_LAG = 2
+SINE_LAG = 1
+PRODUCT_LAG = 3
+SUM_LAG = 4
+STORE_LAG = 5
+COEF_BUFS = 3
+SCALAR_SORTS = (2, 4, 6, 8, 10)
+WORDS = GROUPS * FREQS // 2
 
 FLOPS = 2 * BATCH * X_ROWS * K * W_BLOCKS * P
 
@@ -56,12 +61,30 @@ def tile_ka_attention_heads_mod_pa_kernel(tc, x, lin_w, lin_b, grid, coef, shift
         x_scales = keep.tile([P, x_tiles * P], U8, name="x_scales", align_bytes=64)
         w_codes = keep.tile([P, W_BLOCKS * P], U32, name="w_codes", align_bytes=64)
         w_scales = keep.tile([P, W_BLOCKS * P], U8, name="w_scales", align_bytes=64)
-        coef_sb = keep.tile([P, TILES * SEG, FREQS * GROUPS], BF16, name="coef_sb")
+        coef_words = keep.tile([P, WORDS, TILES * SEG], F32, name="coef_words")
         ident = keep.tile([P, P], F32, name="ident")
-        ident_bf = keep.tile([P, P], BF16, name="ident_bf")
         bias_t = keep.tile([P, W_BLOCKS], F32, name="bias_t")
         turns = keep.tile([P, GROUPS * FREQS], F32, name="turns")
 
+        coef_in = stack.enter_context(tc.tile_pool(name="coef_in", bufs=COEF_BUFS))
+
+        def load_coef(t):
+            raw = coef_in.tile([P, SEG * FREQS * GROUPS], BF16, name="coef_raw")
+            nc.sync.dma_start(out=raw[:], in_=coef_view[t])
+            coef_raw_of[t] = raw
+
+        def sort_coef(t):
+            dst = coef_words[:, :, t * SEG : (t + 1) * SEG]
+            src = coef_raw_of[t][:].bitcast(F32).rearrange("p (d w) -> p w d", w=WORDS)
+            if t in SCALAR_SORTS:
+                nc.scalar.copy(out=dst, in_=src)
+            else:
+                nc.vector.tensor_copy(out=dst, in_=src)
+            if t + COEF_BUFS < TILES:
+                load_coef(t + COEF_BUFS)
+
+        coef_raw_of = {}
+        stack.enter_context(tc.manual_schedule())
         with tc.tile_pool(name="prep", bufs=1) as prep:
             x_raw = prep.tile([P, x_tiles * K], BF16, name="x_raw")
             w_raw = prep.tile([P, W_BLOCKS * K], BF16, name="w_raw")
@@ -73,35 +96,23 @@ def tile_ka_attention_heads_mod_pa_kernel(tc, x, lin_w, lin_b, grid, coef, shift
 
             nc.vector.memset(bias_rows[:], 0.0)
             make_identity(nc, ident[:])
-            make_identity(nc, ident_bf[:])
 
+            nc.scalar.dma_start(out=bias_rows[0:W_BLOCKS, :], in_=lin_b.rearrange("(a d) -> a d", d=P))
+            nc.scalar.dma_start(out=grid_bc[:], in_=grid.rearrange("j m -> (j m)").partition_broadcast(P))
             nc.sync.dma_start(out=x_raw[:].rearrange("p (a k) -> p a k", k=K), in_=x_view)
             for c in range(GROUPS):
                 nc.sync.dma_start(
                     out=w_raw[:, c * 4 * K : (c + 1) * 4 * K].rearrange("p (a k) -> p a k", k=K),
                     in_=w_view[:, c * 4 : (c + 1) * 4, :],
                 )
-            for t in range(TILES):
-                nc.sync.dma_start(
-                    out=coef_sb[:, t * SEG : (t + 1) * SEG, :].rearrange("p d c -> p (d c)"),
-                    in_=coef_view[t],
-                )
-            nc.scalar.dma_start(out=bias_rows[0:W_BLOCKS, :], in_=lin_b.rearrange("(a d) -> a d", d=P))
-            nc.scalar.dma_start(out=grid_bc[:], in_=grid.rearrange("j m -> (j m)").partition_broadcast(P))
 
-            nc.vector.tensor_scalar(
-                out=turns[:], in0=grid_bc[:], scalar1=1.0 / (2.0 * math.pi), scalar2=None, op0=ALU.mult
-            )
+            for t in range(COEF_BUFS):
+                load_coef(t)
 
-            nc.vector.tensor_copy(out=bias_rows_f[:], in_=bias_rows[:])
-            bias_ps = psum_acc.tile([P, UNIT], F32, name="bias_ps", tag="acc")
-            nc.tensor.transpose(bias_ps[:, 0:P], bias_rows_f[:], ident[:])
-            nc.vector.tensor_copy(out=bias_t[:], in_=bias_ps[:, 0:W_BLOCKS])
-
-            def put_k_on_partitions(raw, grouped, n_tiles):
+            def put_k_on_partitions(raw, grouped, pairs):
                 words = raw[:].bitcast(F32)
                 grouped_words = grouped[:].bitcast(F32)
-                for pair in range(n_tiles // 2):
+                for pair in pairs:
                     bank = psum_turn.tile([P, UNIT], F32, name="turned", tag="bank")
                     for a in range(2):
                         for u in range(2):
@@ -115,119 +126,140 @@ def tile_ka_attention_heads_mod_pa_kernel(tc, x, lin_w, lin_b, grid, coef, shift
                         "p (a r u) -> p a r u", a=2, u=2
                     )
                     src = bank[:].rearrange("p (a u r) -> p a r u", a=2, u=2)
-                    if pair % 2 == 0:
-                        nc.vector.tensor_copy(out=dst, in_=src)
-                    else:
-                        nc.scalar.copy(out=dst, in_=src)
+                    nc.scalar.copy(out=dst, in_=src)
 
-            def quantise(grouped, codes, scales, n_rows):
-                for first in range(0, n_rows, 512):
-                    n = min(512, n_rows - first)
-                    nc.vector.quantize_mx(
-                        out=codes[:, first : first + n].bitcast(FP8X4),
-                        scales=scales[:, first : first + n],
-                        in_=grouped[:, first * 4 : (first + n) * 4],
-                    )
+            def quantise(grouped, codes, scales, first, n):
+                nc.vector.quantize_mx(
+                    out=codes[:, first : first + n].bitcast(FP8X4),
+                    scales=scales[:, first : first + n],
+                    in_=grouped[:, first * 4 : (first + n) * 4],
+                )
 
-            put_k_on_partitions(x_raw, x_grouped, x_tiles)
-            put_k_on_partitions(w_raw, w_grouped, W_BLOCKS)
-            quantise(x_grouped, x_codes, x_scales, x_tiles * P)
-            quantise(w_grouped, w_codes, w_scales, W_BLOCKS * P)
+            put_k_on_partitions(x_raw, x_grouped, range(x_tiles // 2))
+            for c in range(GROUPS + 1):
+                if c < GROUPS:
+                    put_k_on_partitions(w_raw, w_grouped, (2 * c, 2 * c + 1))
+                if c == 0:
+                    quantise(x_grouped, x_codes, x_scales, 0, 512)
+                    quantise(x_grouped, x_codes, x_scales, 512, x_tiles * P - 512)
+                else:
+                    quantise(w_grouped, w_codes, w_scales, (c - 1) * 512, 512)
+
+            nc.vector.tensor_scalar(
+                out=turns[:], in0=grid_bc[:], scalar1=1.0 / (2.0 * math.pi), scalar2=None, op0=ALU.mult
+            )
+
+            nc.vector.tensor_copy(out=bias_rows_f[:], in_=bias_rows[:])
+            bias_ps = psum_acc.tile([P, UNIT], F32, name="bias_ps", tag="acc")
+            nc.tensor.transpose(bias_ps[:, 0:P], bias_rows_f[:], ident[:])
+            nc.vector.tensor_copy(out=bias_t[:], in_=bias_ps[:, 0:W_BLOCKS])
 
         loop = stack.enter_context(tc.tile_pool(name="loop", bufs=2))
         halves = GROUPS * FREQS * UNITS
         halves_per_group = FREQS * UNITS
 
-        def project(j):
-            first_row = min((2 * SEG * j) // W_BLOCKS, WINDOW - ROWS)
+        def group_tiles(j):
             shift_sb = loop.tile([P, TILES, SEG], BF16, name="shift_sb")
             nc.sync.dma_start(out=shift_sb[:], in_=shift_view[:, j * TILES : (j + 1) * TILES, :])
             xl_t = loop.tile([P, BATCH, ROWS * W_BLOCKS], F32, name="xl_t")
-            for b in range(BATCH):
-                window = b * X_ROWS + WINDOW_STEP * j
-                for c in range(GROUPS):
-                    acc = psum_acc.tile([P, UNIT], F32, name="acc", tag="acc")
-                    for d in range(4):
-                        a = c * 4 + d
-                        nc.tensor.matmul_mx(
-                            out=acc[:, d * WINDOW : (d + 1) * WINDOW],
-                            lhsT=w_codes[:, a * P : (a + 1) * P].bitcast(FP8X4),
-                            lhsT_scale=w_scales[:, a * P : (a + 1) * P],
-                            rhs=x_codes[:, window : window + WINDOW].bitcast(FP8X4),
-                            rhs_scale=x_scales[:, window : window + WINDOW],
-                            start=True,
-                            stop=True,
-                        )
-                    nc.vector.tensor_tensor(
-                        out=xl_t[:, b, :].rearrange("p (r a) -> p r a", a=W_BLOCKS)[:, :, c * 4 : (c + 1) * 4],
-                        in0=acc[:].rearrange("p (d r) -> p r d", d=4)[:, first_row : first_row + ROWS, :],
-                        in1=bias_t[:, c * 4 : (c + 1) * 4].unsqueeze(1).to_broadcast([P, ROWS, 4]),
-                        op=ALU.add,
-                    )
-            return xl_t, 2 * SEG * j - W_BLOCKS * first_row, shift_sb
+            first_row_of[j] = min((2 * SEG * j) // W_BLOCKS, WINDOW - ROWS)
+            xl_of[j] = xl_t
+            shift_of[j] = shift_sb
 
-        def turn_coef(i):
+        def project_mx(j, piece):
+            c, b = divmod(piece, BATCH)
+            window = b * X_ROWS + WINDOW_STEP * j
+            acc = psum_acc.tile([P, UNIT], F32, name="acc", tag="acc")
+            for d in range(4):
+                a = c * 4 + d
+                nc.tensor.matmul_mx(
+                    out=acc[:, d * WINDOW : (d + 1) * WINDOW],
+                    lhsT=w_codes[:, a * P : (a + 1) * P].bitcast(FP8X4),
+                    lhsT_scale=w_scales[:, a * P : (a + 1) * P],
+                    rhs=x_codes[:, window : window + WINDOW].bitcast(FP8X4),
+                    rhs_scale=x_scales[:, window : window + WINDOW],
+                    start=True,
+                    stop=True,
+                )
+            acc_of[piece] = acc
+
+        def project_bias(j, piece):
+            c, b = divmod(piece, BATCH)
+            first_row = first_row_of[j]
+            nc.vector.tensor_tensor(
+                out=xl_of[j][:, b, :].rearrange("p (r a) -> p r a", a=W_BLOCKS)[:, :, c * 4 : (c + 1) * 4],
+                in0=acc_of[piece][:].rearrange("p (d r) -> p r d", d=4)[:, first_row : first_row + ROWS, :],
+                in1=bias_t[:, c * 4 : (c + 1) * 4].unsqueeze(1).to_broadcast([P, ROWS, 4]),
+                op=ALU.add,
+            )
+
+        def segments(j, unit):
+            first = 2 * SEG * j - W_BLOCKS * first_row_of[j] + unit * UNIT
+            return xl_of[j][:, :, first : first + UNIT]
+
+        def place(i):
             jm, unit = divmod(i, UNITS)
             j, m = divmod(jm, FREQS)
-            column = m * GROUPS + j
-            turned = psum_turn.tile([P, UNIT], BF16, name="coef_ps", tag="bank")
+            return jm, j, m, unit
+
+        def turn_coef(i):
+            jm, j, m, unit = place(i)
+            bank = psum_turn.tile([P, UNIT], F32, name="coef_ps", tag="bank")
             for t in range(UNIT_TILES):
                 first = (unit * UNIT_TILES + t) * SEG
                 nc.tensor.transpose(
-                    turned[:, t * SEG : (t + 1) * SEG], coef_sb[:, first : first + SEG, column], ident_bf[:]
+                    bank[:, t * SEG : (t + 1) * SEG],
+                    coef_words[:, (m * GROUPS + j) // 2, first : first + SEG],
+                    ident[:],
                 )
-            return turned
+            coef_t_of[i] = bank[:].bitcast(BF16).rearrange("p (s e) -> p e s", e=2)[:, (m * GROUPS + j) % 2, :]
 
 
         def xl_of_half(i):
-            xl_t, first_seg = xl_of[i // halves_per_group][0:2]
-            unit = i % UNITS
-            return xl_t[:, :, first_seg + unit * UNIT : first_seg + (unit + 1) * UNIT]
+            jm, j, m, unit = place(i)
+            return segments(j, unit)
 
         def whole_turns(i):
+            jm = place(i)[0]
             whole = loop.tile([P, BATCH, UNIT], I32, name="whole", bufs=WHOLE_AHEAD + 1)
             nc.gpsimd.tensor_scalar(
                 out=whole[:],
                 in0=xl_of_half(i),
-                scalar1=turns[:, i // UNITS : i // UNITS + 1],
+                scalar1=turns[:, jm : jm + 1],
                 scalar2=0.0,
                 op0=ALU.mult,
                 op1=ALU.add,
             )
-            return whole
+            whole_of[i] = whole
 
-        def rest_of_turn(i, whole):
-            rest = loop.tile([P, BATCH, UNIT], F32, name="rest", bufs=3)
+        def rest_of_turn(i):
+            jm = place(i)[0]
+            sine_of[i] = loop.tile([P, BATCH, UNIT], F32, name="sine", bufs=6)
             nc.vector.scalar_tensor_tensor(
-                out=rest[:],
+                out=sine_of[i][:],
                 in0=xl_of_half(i),
-                scalar=turns[:, i // UNITS : i // UNITS + 1],
-                in1=whole[:],
+                scalar=turns[:, jm : jm + 1],
+                in1=whole_of[i][:],
                 op0=ALU.mult,
                 op1=ALU.subtract,
             )
-            return rest
 
-        def sine_of_rest(rest):
-            sine = loop.tile([P, BATCH, UNIT], F32, name="sine", bufs=3)
-            nc.scalar.activation(out=sine[:], in_=rest[:], func=ACT.Sin, scale=2.0 * math.pi)
-            return sine
+        def sine(i):
+            nc.scalar.activation(out=sine_of[i][:], in_=sine_of[i][:], func=ACT.Sin, scale=2.0 * math.pi)
 
-        def four_terms(sine, coef_t):
-            products = loop.tile([P, BATCH, UNIT], F32, name="products", bufs=5)
+        def four_terms(i):
             nc.vector.tensor_tensor(
-                out=products[:],
-                in0=sine[:],
-                in1=coef_t[:].unsqueeze(1).to_broadcast([P, BATCH, UNIT]),
+                out=sine_of[i][:],
+                in0=sine_of[i][:],
+                in1=coef_t_of[i].unsqueeze(1).to_broadcast([P, BATCH, UNIT]),
                 op=ALU.mult,
             )
-            return products
 
         def add_up(block):
-            sums = psum_sums.tile([P, BATCH, SEG], F32, name="sums")
+            sums = psum_sums.tile([P, 2 * BATCH, SEG], F32, name="sums")
             for b in range(BATCH):
                 for e in range(TERMS):
-                    products = products_of[2 * block + e // UNIT_TILES]
+                    products = sine_of[2 * block + e // UNIT_TILES]
                     t = e % UNIT_TILES
                     nc.tensor.matmul(
                         out=sums[:, b, :],
@@ -241,41 +273,52 @@ def tile_ka_attention_heads_mod_pa_kernel(tc, x, lin_w, lin_b, grid, coef, shift
 
         def store(block):
             total = loop.tile([P, BATCH, SEG], F32, name="total")
+            shift_row = shift_of[block // TILES][:, block % TILES : block % TILES + 1, :]
             nc.vector.tensor_tensor(
                 out=total[:],
-                in0=sums_of[block][:],
-                in1=xl_of[block // TILES][2][:, block % TILES : block % TILES + 1, :].to_broadcast([P, BATCH, SEG]),
+                in0=sums_of[block][:, 0:BATCH, :],
+                in1=shift_row.to_broadcast([P, BATCH, SEG]),
                 op=ALU.add,
             )
             nc.sync.dma_start(out=out_view[:, :, block, :], in_=total[:])
 
-        coef_t_of = {}
-        whole_of = {}
-        rest_of = {}
-        sine_of = {}
-        products_of = {}
-        sums_of = {}
-        with tc.manual_schedule():
-            xl_of = {0: project(0)}
-            for i in range(WHOLE_AHEAD):
-                whole_of[i] = whole_turns(i)
-            for i in range(halves + PRODUCT_LAG + STORE_LAG + 1):
-                if i + WHOLE_AHEAD < halves:
-                    whole_of[i + WHOLE_AHEAD] = whole_turns(i + WHOLE_AHEAD)
-                if i < halves:
-                    rest_of[i] = rest_of_turn(i, whole_of[i])
-                if 1 <= i <= halves:
-                    sine_of[i - 1] = sine_of_rest(rest_of[i - 1])
-                if i < halves:
-                    coef_t_of[i] = turn_coef(i)
-                multiplied = i - PRODUCT_LAG
-                if 0 <= multiplied < halves:
-                    products_of[multiplied] = four_terms(sine_of[multiplied], coef_t_of[multiplied])
-                stored = multiplied - STORE_LAG
-                if stored >= 0 and stored % 2 == 1:
-                    store(stored // 2)
-                if 0 <= multiplied < halves and multiplied % 2 == 1:
-                    add_up(multiplied // 2)
-                j, local = divmod(i, halves_per_group)
-                if j + 1 < GROUPS and local == halves_per_group // 2:
-                    xl_of[j + 1] = project(j + 1)
+        first_row_of, xl_of, shift_of, acc_of = {}, {}, {}, {}
+        whole_of, sine_of, coef_t_of, sums_of = {}, {}, {}, {}
+        pieces = BATCH * GROUPS
+        sort_coef(0)
+        group_tiles(0)
+        for piece in range(pieces + 1):
+            if piece < pieces:
+                project_mx(0, piece)
+            if piece >= 1:
+                project_bias(0, piece - 1)
+        sort_coef(1)
+        sort_coef(2)
+        for i in range(WHOLE_AHEAD):
+            whole_turns(i)
+        for i in range(halves + STORE_LAG + 1):
+            if i + WHOLE_AHEAD < halves:
+                whole_turns(i + WHOLE_AHEAD)
+            if i < halves:
+                rest_of_turn(i)
+            if 0 <= i - SINE_LAG < halves:
+                sine(i - SINE_LAG)
+            if 0 <= i - SUM_LAG < halves and (i - SUM_LAG) % 2 == 1:
+                add_up((i - SUM_LAG) // 2)
+            j, local = divmod(i, halves_per_group)
+            if j + 1 < GROUPS:
+                if local == 6:
+                    group_tiles(j + 1)
+                if 8 <= local < 8 + pieces:
+                    project_bias(j + 1, local - 8)
+                if 7 <= local < 7 + pieces:
+                    project_mx(j + 1, local - 7)
+            if 0 <= i - PRODUCT_LAG < halves:
+                four_terms(i - PRODUCT_LAG)
+            if 0 <= i - STORE_LAG < halves and (i - STORE_LAG) % 2 == 1:
+                store((i - STORE_LAG) // 2)
+            for t in (2 * i + 3, 2 * i + 4):
+                if t < TILES:
+                    sort_coef(t)
+            if 0 <= i - PRODUCT_LAG + 1 < halves:
+                turn_coef(i - PRODUCT_LAG + 1)

@@ -31,12 +31,9 @@ ROWS = 78
 TERMS = 8
 WHOLE_AHEAD = 2
 SINE_LAG = 1
-PRODUCT_LAG = 3
-SUM_LAG = 4
-STORE_LAG = 5
-COEF_BUFS = 3
-SCALAR_SORTS = (2, 4, 6, 8, 10)
-WORDS = GROUPS * FREQS // 2
+PRODUCT_LAG = 5
+SUM_LAG = 6
+STORE_LAG = 7
 
 FLOPS = 2 * BATCH * X_ROWS * K * W_BLOCKS * P
 
@@ -61,29 +58,12 @@ def tile_ka_attention_heads_mod_pa_kernel(tc, x, lin_w, lin_b, grid, coef, shift
         x_scales = keep.tile([P, x_tiles * P], U8, name="x_scales", align_bytes=64)
         w_codes = keep.tile([P, W_BLOCKS * P], U32, name="w_codes", align_bytes=64)
         w_scales = keep.tile([P, W_BLOCKS * P], U8, name="w_scales", align_bytes=64)
-        coef_words = keep.tile([P, WORDS, TILES * SEG], F32, name="coef_words")
+        coef_sb = keep.tile([P, TILES * SEG, FREQS * GROUPS], BF16, name="coef_sb")
         ident = keep.tile([P, P], F32, name="ident")
+        ident_bf = keep.tile([P, P], BF16, name="ident_bf")
         bias_t = keep.tile([P, W_BLOCKS], F32, name="bias_t")
         turns = keep.tile([P, GROUPS * FREQS], F32, name="turns")
 
-        coef_in = stack.enter_context(tc.tile_pool(name="coef_in", bufs=COEF_BUFS))
-
-        def load_coef(t):
-            raw = coef_in.tile([P, SEG * FREQS * GROUPS], BF16, name="coef_raw")
-            nc.sync.dma_start(out=raw[:], in_=coef_view[t])
-            coef_raw_of[t] = raw
-
-        def sort_coef(t):
-            dst = coef_words[:, :, t * SEG : (t + 1) * SEG]
-            src = coef_raw_of[t][:].bitcast(F32).rearrange("p (d w) -> p w d", w=WORDS)
-            if t in SCALAR_SORTS:
-                nc.scalar.copy(out=dst, in_=src)
-            else:
-                nc.vector.tensor_copy(out=dst, in_=src)
-            if t + COEF_BUFS < TILES:
-                load_coef(t + COEF_BUFS)
-
-        coef_raw_of = {}
         stack.enter_context(tc.manual_schedule())
         with tc.tile_pool(name="prep", bufs=1) as prep:
             x_raw = prep.tile([P, x_tiles * K], BF16, name="x_raw")
@@ -96,6 +76,7 @@ def tile_ka_attention_heads_mod_pa_kernel(tc, x, lin_w, lin_b, grid, coef, shift
 
             nc.vector.memset(bias_rows[:], 0.0)
             make_identity(nc, ident[:])
+            make_identity(nc, ident_bf[:])
 
             nc.scalar.dma_start(out=bias_rows[0:W_BLOCKS, :], in_=lin_b.rearrange("(a d) -> a d", d=P))
             nc.scalar.dma_start(out=grid_bc[:], in_=grid.rearrange("j m -> (j m)").partition_broadcast(P))
@@ -106,8 +87,11 @@ def tile_ka_attention_heads_mod_pa_kernel(tc, x, lin_w, lin_b, grid, coef, shift
                     in_=w_view[:, c * 4 : (c + 1) * 4, :],
                 )
 
-            for t in range(COEF_BUFS):
-                load_coef(t)
+            for t in range(TILES):
+                nc.sync.dma_start(
+                    out=coef_sb[:, t * SEG : (t + 1) * SEG, :].rearrange("p d c -> p (d c)"),
+                    in_=coef_view[t],
+                )
 
             def put_k_on_partitions(raw, grouped, pairs):
                 words = raw[:].bitcast(F32)
@@ -204,15 +188,13 @@ def tile_ka_attention_heads_mod_pa_kernel(tc, x, lin_w, lin_b, grid, coef, shift
 
         def turn_coef(i):
             jm, j, m, unit = place(i)
-            bank = psum_turn.tile([P, UNIT], F32, name="coef_ps", tag="bank")
+            bank = psum_turn.tile([P, 2 * UNIT], BF16, name="coef_ps", tag="bank")
             for t in range(UNIT_TILES):
                 first = (unit * UNIT_TILES + t) * SEG
                 nc.tensor.transpose(
-                    bank[:, t * SEG : (t + 1) * SEG],
-                    coef_words[:, (m * GROUPS + j) // 2, first : first + SEG],
-                    ident[:],
+                    bank[:, t * SEG : (t + 1) * SEG], coef_sb[:, first : first + SEG, m * GROUPS + j], ident_bf[:]
                 )
-            coef_t_of[i] = bank[:].bitcast(BF16).rearrange("p (s e) -> p e s", e=2)[:, (m * GROUPS + j) % 2, :]
+            coef_t_of[i] = bank[:, 0:UNIT]
 
 
         def xl_of_half(i):
@@ -234,7 +216,7 @@ def tile_ka_attention_heads_mod_pa_kernel(tc, x, lin_w, lin_b, grid, coef, shift
 
         def rest_of_turn(i):
             jm = place(i)[0]
-            sine_of[i] = loop.tile([P, BATCH, UNIT], F32, name="sine", bufs=6)
+            sine_of[i] = loop.tile([P, BATCH, UNIT], F32, name="sine", bufs=9)
             nc.vector.scalar_tensor_tensor(
                 out=sine_of[i][:],
                 in0=xl_of_half(i),
@@ -285,15 +267,12 @@ def tile_ka_attention_heads_mod_pa_kernel(tc, x, lin_w, lin_b, grid, coef, shift
         first_row_of, xl_of, shift_of, acc_of = {}, {}, {}, {}
         whole_of, sine_of, coef_t_of, sums_of = {}, {}, {}, {}
         pieces = BATCH * GROUPS
-        sort_coef(0)
         group_tiles(0)
         for piece in range(pieces + 1):
             if piece < pieces:
                 project_mx(0, piece)
             if piece >= 1:
                 project_bias(0, piece - 1)
-        sort_coef(1)
-        sort_coef(2)
         for i in range(WHOLE_AHEAD):
             whole_turns(i)
         for i in range(halves + STORE_LAG + 1):
@@ -307,18 +286,15 @@ def tile_ka_attention_heads_mod_pa_kernel(tc, x, lin_w, lin_b, grid, coef, shift
                 add_up((i - SUM_LAG) // 2)
             j, local = divmod(i, halves_per_group)
             if j + 1 < GROUPS:
-                if local == 6:
+                if local == 9:
                     group_tiles(j + 1)
-                if 8 <= local < 8 + pieces:
-                    project_bias(j + 1, local - 8)
-                if 7 <= local < 7 + pieces:
-                    project_mx(j + 1, local - 7)
+                if 11 <= local < 11 + pieces:
+                    project_bias(j + 1, local - 11)
+                if 10 <= local < 10 + pieces:
+                    project_mx(j + 1, local - 10)
             if 0 <= i - PRODUCT_LAG < halves:
                 four_terms(i - PRODUCT_LAG)
             if 0 <= i - STORE_LAG < halves and (i - STORE_LAG) % 2 == 1:
                 store((i - STORE_LAG) // 2)
-            for t in (2 * i + 3, 2 * i + 4):
-                if t < TILES:
-                    sort_coef(t)
             if 0 <= i - PRODUCT_LAG + 1 < halves:
                 turn_coef(i - PRODUCT_LAG + 1)

@@ -34,6 +34,12 @@ SINE_LAG = 1
 PRODUCT_LAG = 5
 SUM_LAG = 6
 STORE_LAG = 7
+SHIFT_AHEAD = 2
+
+PART = SEG // 2
+PARTS_AHEAD = 6
+WORDS = GROUPS * FREQS // 2
+TILE_WORDS = SEG * WORDS
 
 FLOPS = 2 * BATCH * X_ROWS * K * W_BLOCKS * P
 
@@ -58,12 +64,28 @@ def tile_ka_attention_heads_mod_pa_kernel(tc, x, lin_w, lin_b, grid, coef, shift
         x_scales = keep.tile([P, x_tiles * P], U8, name="x_scales", align_bytes=64)
         w_codes = keep.tile([P, W_BLOCKS * P], U32, name="w_codes", align_bytes=64)
         w_scales = keep.tile([P, W_BLOCKS * P], U8, name="w_scales", align_bytes=64)
-        coef_sb = keep.tile([P, TILES * SEG, FREQS * GROUPS], BF16, name="coef_sb")
+        coef_sb = keep.tile([P, (TILES + 1) * TILE_WORDS * 2], BF16, name="coef_sb")
         ident = keep.tile([P, P], F32, name="ident")
         ident_bf = keep.tile([P, P], BF16, name="ident_bf")
         bias_t = keep.tile([P, W_BLOCKS], F32, name="bias_t")
         turns = keep.tile([P, GROUPS * FREQS], F32, name="turns")
 
+        def coef_place(t):
+            return coef_sb[:, t * TILE_WORDS * 2 : (t + 1) * TILE_WORDS * 2]
+
+        def sort_coef(part):
+            t, s = divmod(part, 2)
+            values = slice(s * PART, (s + 1) * PART)
+            nc.scalar.copy(
+                out=coef_place(t).bitcast(F32).rearrange("p (g r d) -> p g d r", r=4, d=SEG)[:, :, values, :],
+                in_=coef_place(t + 1).bitcast(F32).rearrange("p (d g r) -> p g d r", r=4, d=SEG)[:, :, values, :],
+            )
+            sorted_parts.add(part)
+
+        def is_laid_out(t):
+            return 2 * min(t + 1, TILES - 1) in sorted_parts and 2 * t + 1 in sorted_parts
+
+        sorted_parts = set()
         stack.enter_context(tc.manual_schedule())
         with tc.tile_pool(name="prep", bufs=1) as prep:
             x_raw = prep.tile([P, x_tiles * K], BF16, name="x_raw")
@@ -87,10 +109,12 @@ def tile_ka_attention_heads_mod_pa_kernel(tc, x, lin_w, lin_b, grid, coef, shift
                     in_=w_view[:, c * 4 : (c + 1) * 4, :],
                 )
 
+            shift_of = {0: keep.tile([P, TILES, SEG], BF16, name="shift_sb", bufs=2)}
             for t in range(TILES):
+                if t == UNIT_TILES:
+                    nc.sync.dma_start(out=shift_of[0][:], in_=shift_view[:, 0:TILES, :])
                 nc.sync.dma_start(
-                    out=coef_sb[:, t * SEG : (t + 1) * SEG, :].rearrange("p d c -> p (d c)"),
-                    in_=coef_view[t],
+                    out=coef_sb[:, (t + 1) * TILE_WORDS * 2 : (t + 2) * TILE_WORDS * 2], in_=coef_view[t]
                 )
 
             def put_k_on_partitions(raw, grouped, pairs):
@@ -143,12 +167,13 @@ def tile_ka_attention_heads_mod_pa_kernel(tc, x, lin_w, lin_b, grid, coef, shift
         halves_per_group = FREQS * UNITS
 
         def group_tiles(j):
-            shift_sb = loop.tile([P, TILES, SEG], BF16, name="shift_sb")
-            nc.sync.dma_start(out=shift_sb[:], in_=shift_view[:, j * TILES : (j + 1) * TILES, :])
             xl_t = loop.tile([P, BATCH, ROWS * W_BLOCKS], F32, name="xl_t")
             first_row_of[j] = min((2 * SEG * j) // W_BLOCKS, WINDOW - ROWS)
             xl_of[j] = xl_t
-            shift_of[j] = shift_sb
+
+        def load_shift(j):
+            shift_of[j] = keep.tile([P, TILES, SEG], BF16, name="shift_sb", bufs=2)
+            nc.sync.dma_start(out=shift_of[j][:], in_=shift_view[:, j * TILES : (j + 1) * TILES, :])
 
         def project_mx(j, piece):
             c, b = divmod(piece, BATCH)
@@ -188,12 +213,15 @@ def tile_ka_attention_heads_mod_pa_kernel(tc, x, lin_w, lin_b, grid, coef, shift
 
         def turn_coef(i):
             jm, j, m, unit = place(i)
+            column = m * GROUPS + j
             bank = psum_turn.tile([P, 2 * UNIT], BF16, name="coef_ps", tag="bank")
             for t in range(UNIT_TILES):
-                first = (unit * UNIT_TILES + t) * SEG
-                nc.tensor.transpose(
-                    bank[:, t * SEG : (t + 1) * SEG], coef_sb[:, first : first + SEG, m * GROUPS + j], ident_bf[:]
-                )
+                tile = unit * UNIT_TILES + t
+                if is_laid_out(tile):
+                    values = coef_place(tile).rearrange("p (w d e) -> p w e d", w=WORDS, e=2)[:, column // 2, column % 2, :]
+                else:
+                    values = coef_place(tile + 1).rearrange("p (d c) -> p c d", d=SEG)[:, column, :]
+                nc.tensor.transpose(bank[:, t * SEG : (t + 1) * SEG], values, ident_bf[:])
             coef_t_of[i] = bank[:, 0:UNIT]
 
 
@@ -240,31 +268,39 @@ def tile_ka_attention_heads_mod_pa_kernel(tc, x, lin_w, lin_b, grid, coef, shift
         def add_up(block):
             sums = psum_sums.tile([P, 2 * BATCH, SEG], F32, name="sums")
             for b in range(BATCH):
+                terms = [shift_t_of[block // 2][:, block % 2, :]]
                 for e in range(TERMS):
                     products = sine_of[2 * block + e // UNIT_TILES]
                     t = e % UNIT_TILES
+                    terms.append(products[:, b, t * SEG : (t + 1) * SEG])
+                for n, term in enumerate(terms):
                     nc.tensor.matmul(
                         out=sums[:, b, :],
-                        lhsT=products[:, b, t * SEG : (t + 1) * SEG],
+                        lhsT=term,
                         rhs=ident[:],
                         is_transpose=True,
-                        start=(e == 0),
-                        stop=(e == TERMS - 1),
+                        start=(n == 0),
+                        stop=(n == TERMS),
                     )
             sums_of[block] = sums
 
+        def turn_shift(pair):
+            bank = psum_acc.tile([P, 2 * UNIT], BF16, name="shift_ps", tag="acc")
+            for n in range(2):
+                block = 2 * pair + n
+                nc.tensor.transpose(
+                    bank[:, n * SEG : (n + 1) * SEG], shift_of[block // TILES][:, block % TILES, :], ident_bf[:]
+                )
+            shift_t_of[pair] = loop.tile([P, 2, SEG], F32, name="shift_t", bufs=3)
+            nc.scalar.copy(out=shift_t_of[pair][:], in_=bank[:, 0 : 2 * SEG].rearrange("p (n q) -> p n q", n=2))
+
         def store(block):
             total = loop.tile([P, BATCH, SEG], F32, name="total")
-            shift_row = shift_of[block // TILES][:, block % TILES : block % TILES + 1, :]
-            nc.vector.tensor_tensor(
-                out=total[:],
-                in0=sums_of[block][:, 0:BATCH, :],
-                in1=shift_row.to_broadcast([P, BATCH, SEG]),
-                op=ALU.add,
-            )
+            nc.scalar.copy(out=total[:], in_=sums_of[block][:, 0:BATCH, :])
             nc.sync.dma_start(out=out_view[:, :, block, :], in_=total[:])
 
-        first_row_of, xl_of, shift_of, acc_of = {}, {}, {}, {}
+        shift_t_of = {}
+        first_row_of, xl_of, acc_of = {}, {}, {}
         whole_of, sine_of, coef_t_of, sums_of = {}, {}, {}, {}
         pieces = BATCH * GROUPS
         group_tiles(0)
@@ -273,6 +309,8 @@ def tile_ka_attention_heads_mod_pa_kernel(tc, x, lin_w, lin_b, grid, coef, shift
                 project_mx(0, piece)
             if piece >= 1:
                 project_bias(0, piece - 1)
+        for part in range(PARTS_AHEAD):
+            sort_coef(part)
         for i in range(WHOLE_AHEAD):
             whole_turns(i)
         for i in range(halves + STORE_LAG + 1):
@@ -282,19 +320,25 @@ def tile_ka_attention_heads_mod_pa_kernel(tc, x, lin_w, lin_b, grid, coef, shift
                 rest_of_turn(i)
             if 0 <= i - SINE_LAG < halves:
                 sine(i - SINE_LAG)
+            if 0 <= i - STORE_LAG < halves and (i - STORE_LAG) % 2 == 1:
+                store((i - STORE_LAG) // 2)
+            ending = i - SUM_LAG + SHIFT_AHEAD
+            if 0 <= ending < halves and ending % 4 == 1:
+                turn_shift(ending // 4)
             if 0 <= i - SUM_LAG < halves and (i - SUM_LAG) % 2 == 1:
                 add_up((i - SUM_LAG) // 2)
             j, local = divmod(i, halves_per_group)
             if j + 1 < GROUPS:
                 if local == 9:
                     group_tiles(j + 1)
+                    load_shift(j + 1)
                 if 11 <= local < 11 + pieces:
                     project_bias(j + 1, local - 11)
                 if 10 <= local < 10 + pieces:
                     project_mx(j + 1, local - 10)
             if 0 <= i - PRODUCT_LAG < halves:
                 four_terms(i - PRODUCT_LAG)
-            if 0 <= i - STORE_LAG < halves and (i - STORE_LAG) % 2 == 1:
-                store((i - STORE_LAG) // 2)
+            if PARTS_AHEAD + i < 2 * TILES:
+                sort_coef(PARTS_AHEAD + i)
             if 0 <= i - PRODUCT_LAG + 1 < halves:
                 turn_coef(i - PRODUCT_LAG + 1)

@@ -29,17 +29,21 @@ WINDOW = 128
 WINDOW_STEP = 64
 ROWS = 78
 TERMS = 8
-WHOLE_AHEAD = 2
+WHOLE_AHEAD = 3
 SINE_LAG = 1
-PRODUCT_LAG = 5
-SUM_LAG = 6
-STORE_LAG = 7
+PRODUCT_LAG = 4
+SUM_LAG = 5
+STORE_LAG = 6
 SHIFT_AHEAD = 2
 
 PART = SEG // 2
 PARTS_AHEAD = 6
 WORDS = GROUPS * FREQS // 2
 TILE_WORDS = SEG * WORDS
+
+FIRST_RESIDENT = 6
+SINE_BUFS = 10
+SHIFT_PAIRS = 3
 
 FLOPS = 2 * BATCH * X_ROWS * K * W_BLOCKS * P
 
@@ -55,9 +59,10 @@ def tile_ka_attention_heads_mod_pa_kernel(tc, x, lin_w, lin_b, grid, coef, shift
 
     with ExitStack() as stack:
         keep = stack.enter_context(tc.tile_pool(name="keep", bufs=1))
-        psum_turn = stack.enter_context(tc.psum_pool(name="psum_turn", bufs=4))
+        psum_turn = stack.enter_context(tc.psum_pool(name="psum_turn", bufs=3))
         psum_acc = stack.enter_context(tc.psum_pool(name="psum_acc", bufs=2))
-        psum_sums = stack.enter_context(tc.psum_pool(name="psum_sums", bufs=2))
+        psum_sums = stack.enter_context(tc.psum_pool(name="psum_sums", bufs=1))
+        psum_xl = stack.enter_context(tc.psum_pool(name="psum_xl", bufs=BATCH))
 
         x_tiles = BATCH * X_ROWS // P
         x_codes = keep.tile([P, x_tiles * P], U32, name="x_codes", align_bytes=64)
@@ -86,6 +91,12 @@ def tile_ka_attention_heads_mod_pa_kernel(tc, x, lin_w, lin_b, grid, coef, shift
             return 2 * min(t + 1, TILES - 1) in sorted_parts and 2 * t + 1 in sorted_parts
 
         sorted_parts = set()
+        shift_of = {}
+
+        def load_shift(pair):
+            shift_of[pair] = keep.tile([P, 2, SEG], BF16, name="shift_sb", bufs=SHIFT_PAIRS)
+            nc.sync.dma_start(out=shift_of[pair][:], in_=shift_view[:, 2 * pair : 2 * pair + 2, :])
+
         stack.enter_context(tc.manual_schedule())
         with tc.tile_pool(name="prep", bufs=1) as prep:
             x_raw = prep.tile([P, x_tiles * K], BF16, name="x_raw")
@@ -109,10 +120,10 @@ def tile_ka_attention_heads_mod_pa_kernel(tc, x, lin_w, lin_b, grid, coef, shift
                     in_=w_view[:, c * 4 : (c + 1) * 4, :],
                 )
 
-            shift_of = {0: keep.tile([P, TILES, SEG], BF16, name="shift_sb", bufs=2)}
             for t in range(TILES):
                 if t == UNIT_TILES:
-                    nc.sync.dma_start(out=shift_of[0][:], in_=shift_view[:, 0:TILES, :])
+                    for pair in range(SHIFT_PAIRS - 1):
+                        load_shift(pair)
                 nc.sync.dma_start(
                     out=coef_sb[:, (t + 1) * TILE_WORDS * 2 : (t + 2) * TILE_WORDS * 2], in_=coef_view[t]
                 )
@@ -171,10 +182,6 @@ def tile_ka_attention_heads_mod_pa_kernel(tc, x, lin_w, lin_b, grid, coef, shift
             first_row_of[j] = min((2 * SEG * j) // W_BLOCKS, WINDOW - ROWS)
             xl_of[j] = xl_t
 
-        def load_shift(j):
-            shift_of[j] = keep.tile([P, TILES, SEG], BF16, name="shift_sb", bufs=2)
-            nc.sync.dma_start(out=shift_of[j][:], in_=shift_view[:, j * TILES : (j + 1) * TILES, :])
-
         def project_mx(j, piece):
             c, b = divmod(piece, BATCH)
             window = b * X_ROWS + WINDOW_STEP * j
@@ -206,8 +213,32 @@ def tile_ka_attention_heads_mod_pa_kernel(tc, x, lin_w, lin_b, grid, coef, shift
             first = 2 * SEG * j - W_BLOCKS * first_row_of[j] + unit * UNIT
             return xl_of[j][:, :, first : first + UNIT]
 
+        def new_sine():
+            return loop.tile([P, BATCH, UNIT], F32, name="sine", bufs=SINE_BUFS)
+
+        def lay_naturally(j, b):
+            if b == 0:
+                x_nat_of[j] = new_sine()
+            bank = psum_turn.tile([P, UNIT], F32, name="turned", tag="bank")
+            for t in range(UNIT_TILES):
+                tile = slice(t * SEG, (t + 1) * SEG)
+                nc.tensor.transpose(bank[:, tile], segments(j, 0)[:, b, tile], ident[:])
+            nc.scalar.copy(out=x_nat_of[j][:, b, :], in_=bank[:])
+
+        def make_resident(j, b):
+            bank = psum_xl.tile([P, UNIT], F32, name="xl_ps")
+            for t in range(UNIT_TILES):
+                tile = slice(t * SEG, (t + 1) * SEG)
+                nc.tensor.transpose(bank[:, tile], x_nat_of[j][:, b, tile], ident[:])
+            resident_of[j, b] = bank
+
+        order = [0, 1, 3, 4, 2, 5] + list(range(6, halves))
+        block_ended = {}
+        for block in range(halves // 2):
+            block_ended[max(order.index(2 * block), order.index(2 * block + 1))] = block
+
         def place(i):
-            jm, unit = divmod(i, UNITS)
+            jm, unit = divmod(order[i], UNITS)
             j, m = divmod(jm, FREQS)
             return jm, j, m, unit
 
@@ -243,16 +274,24 @@ def tile_ka_attention_heads_mod_pa_kernel(tc, x, lin_w, lin_b, grid, coef, shift
             whole_of[i] = whole
 
         def rest_of_turn(i):
-            jm = place(i)[0]
-            sine_of[i] = loop.tile([P, BATCH, UNIT], F32, name="sine", bufs=9)
-            nc.vector.scalar_tensor_tensor(
-                out=sine_of[i][:],
-                in0=xl_of_half(i),
-                scalar=turns[:, jm : jm + 1],
-                in1=whole_of[i][:],
-                op0=ALU.mult,
-                op1=ALU.subtract,
-            )
+            jm, j, m, unit = place(i)
+            sine_of[i] = new_sine()
+
+            def subtract(where, xl):
+                nc.vector.scalar_tensor_tensor(
+                    out=sine_of[i][where],
+                    in0=xl,
+                    scalar=turns[:, jm : jm + 1],
+                    in1=whole_of[i][where],
+                    op0=ALU.mult,
+                    op1=ALU.subtract,
+                )
+
+            if unit == 0 and i >= FIRST_RESIDENT:
+                for b in range(BATCH):
+                    subtract((slice(None), b, slice(None)), resident_of[j, b][:])
+            else:
+                subtract(slice(None), segments(j, unit))
 
         def sine(i):
             nc.scalar.activation(out=sine_of[i][:], in_=sine_of[i][:], func=ACT.Sin, scale=2.0 * math.pi)
@@ -270,7 +309,7 @@ def tile_ka_attention_heads_mod_pa_kernel(tc, x, lin_w, lin_b, grid, coef, shift
             for b in range(BATCH):
                 terms = [shift_t_of[block // 2][:, block % 2, :]]
                 for e in range(TERMS):
-                    products = sine_of[2 * block + e // UNIT_TILES]
+                    products = sine_of[order.index(2 * block + e // UNIT_TILES)]
                     t = e % UNIT_TILES
                     terms.append(products[:, b, t * SEG : (t + 1) * SEG])
                 for n, term in enumerate(terms):
@@ -287,10 +326,9 @@ def tile_ka_attention_heads_mod_pa_kernel(tc, x, lin_w, lin_b, grid, coef, shift
         def turn_shift(pair):
             bank = psum_acc.tile([P, 2 * UNIT], BF16, name="shift_ps", tag="acc")
             for n in range(2):
-                block = 2 * pair + n
-                nc.tensor.transpose(
-                    bank[:, n * SEG : (n + 1) * SEG], shift_of[block // TILES][:, block % TILES, :], ident_bf[:]
-                )
+                nc.tensor.transpose(bank[:, n * SEG : (n + 1) * SEG], shift_of[pair][:, n, :], ident_bf[:])
+            if pair + SHIFT_PAIRS - 1 < halves // 4:
+                load_shift(pair + SHIFT_PAIRS - 1)
             shift_t_of[pair] = loop.tile([P, 2, SEG], F32, name="shift_t", bufs=3)
             nc.scalar.copy(out=shift_t_of[pair][:], in_=bank[:, 0 : 2 * SEG].rearrange("p (n q) -> p n q", n=2))
 
@@ -300,7 +338,12 @@ def tile_ka_attention_heads_mod_pa_kernel(tc, x, lin_w, lin_b, grid, coef, shift
             nc.sync.dma_start(out=out_view[:, :, block, :], in_=total[:])
 
         shift_t_of = {}
-        first_row_of, xl_of, acc_of = {}, {}, {}
+        def subtracted_in_step(i):
+            if i < FIRST_RESIDENT or i == FIRST_RESIDENT:
+                return [i]
+            return [i, i + 1, i + 2] if i % UNITS == 1 else []
+
+        first_row_of, xl_of, acc_of, x_nat_of, resident_of = {}, {}, {}, {}, {}
         whole_of, sine_of, coef_t_of, sums_of = {}, {}, {}, {}
         pieces = BATCH * GROUPS
         group_tiles(0)
@@ -316,29 +359,38 @@ def tile_ka_attention_heads_mod_pa_kernel(tc, x, lin_w, lin_b, grid, coef, shift
         for i in range(halves + STORE_LAG + 1):
             if i + WHOLE_AHEAD < halves:
                 whole_turns(i + WHOLE_AHEAD)
-            if i < halves:
-                rest_of_turn(i)
+            if i - STORE_LAG in block_ended:
+                store(block_ended[i - STORE_LAG])
+            for n in subtracted_in_step(i):
+                if n < halves:
+                    rest_of_turn(n)
             if 0 <= i - SINE_LAG < halves:
                 sine(i - SINE_LAG)
-            if 0 <= i - STORE_LAG < halves and (i - STORE_LAG) % 2 == 1:
-                store((i - STORE_LAG) // 2)
+            if 0 <= i - PRODUCT_LAG + 1 < halves:
+                turn_coef(i - PRODUCT_LAG + 1)
             ending = i - SUM_LAG + SHIFT_AHEAD
             if 0 <= ending < halves and ending % 4 == 1:
                 turn_shift(ending // 4)
-            if 0 <= i - SUM_LAG < halves and (i - SUM_LAG) % 2 == 1:
-                add_up((i - SUM_LAG) // 2)
+            if i - SUM_LAG in block_ended:
+                add_up(block_ended[i - SUM_LAG])
             j, local = divmod(i, halves_per_group)
             if j + 1 < GROUPS:
-                if local == 9:
+                first_piece = 0 if j == 0 else 6
+                if local == first_piece:
                     group_tiles(j + 1)
-                    load_shift(j + 1)
-                if 11 <= local < 11 + pieces:
-                    project_bias(j + 1, local - 11)
-                if 10 <= local < 10 + pieces:
-                    project_mx(j + 1, local - 10)
+                if first_piece < local <= first_piece + pieces:
+                    project_bias(j + 1, local - first_piece - 1)
+                if first_piece <= local < first_piece + pieces:
+                    project_mx(j + 1, local - first_piece)
+                if 17 <= local < 17 + BATCH:
+                    lay_naturally(j + 1, local - 17)
+                if 20 <= local < 20 + BATCH:
+                    make_resident(j + 1, local - 20)
+            if FIRST_RESIDENT - 4 <= i < FIRST_RESIDENT - 2:
+                lay_naturally(0, i - FIRST_RESIDENT + 4)
+            if FIRST_RESIDENT - 2 <= i < FIRST_RESIDENT:
+                make_resident(0, i - FIRST_RESIDENT + 2)
             if 0 <= i - PRODUCT_LAG < halves:
                 four_terms(i - PRODUCT_LAG)
             if PARTS_AHEAD + i < 2 * TILES:
                 sort_coef(PARTS_AHEAD + i)
-            if 0 <= i - PRODUCT_LAG + 1 < halves:
-                turn_coef(i - PRODUCT_LAG + 1)

@@ -41,6 +41,7 @@ PARTS_AHEAD = 6
 WORDS = GROUPS * FREQS // 2
 TILE_WORDS = SEG * WORDS
 
+VECTOR_TURNS = 6
 FIRST_RESIDENT = 6
 SINE_BUFS = 10
 SHIFT_PAIRS = 3
@@ -97,6 +98,41 @@ def tile_ka_attention_heads_mod_pa_kernel(tc, x, lin_w, lin_b, grid, coef, shift
             shift_of[pair] = keep.tile([P, 2, SEG], BF16, name="shift_sb", bufs=SHIFT_PAIRS)
             nc.sync.dma_start(out=shift_of[pair][:], in_=shift_view[:, 2 * pair : 2 * pair + 2, :])
 
+        xl_pool = stack.enter_context(tc.tile_pool(name="xl", bufs=2))
+        first_row_of, xl_of, acc_of = {}, {}, {}
+
+        def group_tiles(j):
+            xl_t = xl_pool.tile([P, BATCH, ROWS * W_BLOCKS], F32, name="xl_t")
+            first_row_of[j] = min((2 * SEG * j) // W_BLOCKS, WINDOW - ROWS)
+            xl_of[j] = xl_t
+
+        def project_mx(j, piece):
+            c, b = divmod(piece, BATCH)
+            window = b * X_ROWS + WINDOW_STEP * j
+            acc = psum_acc.tile([P, UNIT], F32, name="acc", tag="acc")
+            for d in range(4):
+                a = c * 4 + d
+                nc.tensor.matmul_mx(
+                    out=acc[:, d * WINDOW : (d + 1) * WINDOW],
+                    lhsT=w_codes[:, a * P : (a + 1) * P].bitcast(FP8X4),
+                    lhsT_scale=w_scales[:, a * P : (a + 1) * P],
+                    rhs=x_codes[:, window : window + WINDOW].bitcast(FP8X4),
+                    rhs_scale=x_scales[:, window : window + WINDOW],
+                    start=True,
+                    stop=True,
+                )
+            acc_of[piece] = acc
+
+        def project_bias(j, piece):
+            c, b = divmod(piece, BATCH)
+            first_row = first_row_of[j]
+            nc.vector.tensor_tensor(
+                out=xl_of[j][:, b, :].rearrange("p (r a) -> p r a", a=W_BLOCKS)[:, :, c * 4 : (c + 1) * 4],
+                in0=acc_of[piece][:].rearrange("p (d r) -> p r d", d=4)[:, first_row : first_row + ROWS, :],
+                in1=bias_t[:, c * 4 : (c + 1) * 4].unsqueeze(1).to_broadcast([P, ROWS, 4]),
+                op=ALU.add,
+            )
+
         stack.enter_context(tc.manual_schedule())
         with tc.tile_pool(name="prep", bufs=1) as prep:
             x_raw = prep.tile([P, x_tiles * K], BF16, name="x_raw")
@@ -105,14 +141,17 @@ def tile_ka_attention_heads_mod_pa_kernel(tc, x, lin_w, lin_b, grid, coef, shift
             w_grouped = prep.tile([P, W_BLOCKS * P * 4], BF16, name="w_grouped", align_bytes=64)
             bias_rows = prep.tile([P, P], BF16, name="bias_rows")
             bias_rows_f = prep.tile([P, P], F32, name="bias_rows_f")
-            grid_bc = prep.tile([P, GROUPS * FREQS], BF16, name="grid_bc")
+            grid_row = prep.tile([P, GROUPS * FREQS], BF16, name="grid_row")
+            ones = prep.tile([P, P], BF16, name="ones")
 
             nc.vector.memset(bias_rows[:], 0.0)
+            nc.vector.memset(grid_row[:], 0.0)
+            nc.vector.memset(ones[:], 1.0)
             make_identity(nc, ident[:])
             make_identity(nc, ident_bf[:])
 
             nc.scalar.dma_start(out=bias_rows[0:W_BLOCKS, :], in_=lin_b.rearrange("(a d) -> a d", d=P))
-            nc.scalar.dma_start(out=grid_bc[:], in_=grid.rearrange("j m -> (j m)").partition_broadcast(P))
+            nc.scalar.dma_start(out=grid_row[0:1, :], in_=grid.rearrange("(o j) m -> o (j m)", o=1))
             nc.sync.dma_start(out=x_raw[:].rearrange("p (a k) -> p a k", k=K), in_=x_view)
             for c in range(GROUPS):
                 nc.sync.dma_start(
@@ -155,59 +194,42 @@ def tile_ka_attention_heads_mod_pa_kernel(tc, x, lin_w, lin_b, grid, coef, shift
                 )
 
             put_k_on_partitions(x_raw, x_grouped, range(x_tiles // 2))
-            for c in range(GROUPS + 1):
+            group_tiles(0)
+            for c in range(GROUPS + 3):
                 if c < GROUPS:
                     put_k_on_partitions(w_raw, w_grouped, (2 * c, 2 * c + 1))
                 if c == 0:
                     quantise(x_grouped, x_codes, x_scales, 0, 512)
                     quantise(x_grouped, x_codes, x_scales, 512, x_tiles * P - 512)
-                else:
+                elif c <= GROUPS:
                     quantise(w_grouped, w_codes, w_scales, (c - 1) * 512, 512)
+                if c == 2:
+                    nc.vector.tensor_copy(out=bias_rows_f[:], in_=bias_rows[:])
+                    bias_ps = psum_turn.tile([P, UNIT], F32, name="bias_ps", tag="bank")
+                    nc.tensor.transpose(bias_ps[:, 0:P], bias_rows_f[:], ident[:])
+                    nc.vector.tensor_copy(out=bias_t[:], in_=bias_ps[:, 0:W_BLOCKS])
+                for b in range(BATCH):
+                    if c >= 3:
+                        project_bias(0, (c - 3) * BATCH + b)
+                for b in range(BATCH):
+                    if 2 <= c < GROUPS + 2:
+                        project_mx(0, (c - 2) * BATCH + b)
 
-            nc.vector.tensor_scalar(
-                out=turns[:], in0=grid_bc[:], scalar1=1.0 / (2.0 * math.pi), scalar2=None, op0=ALU.mult
+            grid_ps = psum_turn.tile([P, UNIT], F32, name="grid_ps", tag="bank")
+            nc.tensor.matmul(
+                out=grid_ps[:, 0 : GROUPS * FREQS], lhsT=ones[:], rhs=grid_row[:], start=True, stop=True
             )
-
-            nc.vector.tensor_copy(out=bias_rows_f[:], in_=bias_rows[:])
-            bias_ps = psum_acc.tile([P, UNIT], F32, name="bias_ps", tag="acc")
-            nc.tensor.transpose(bias_ps[:, 0:P], bias_rows_f[:], ident[:])
-            nc.vector.tensor_copy(out=bias_t[:], in_=bias_ps[:, 0:W_BLOCKS])
+            nc.vector.tensor_scalar(
+                out=turns[:],
+                in0=grid_ps[:, 0 : GROUPS * FREQS],
+                scalar1=1.0 / (2.0 * math.pi),
+                scalar2=None,
+                op0=ALU.mult,
+            )
 
         loop = stack.enter_context(tc.tile_pool(name="loop", bufs=2))
         halves = GROUPS * FREQS * UNITS
         halves_per_group = FREQS * UNITS
-
-        def group_tiles(j):
-            xl_t = loop.tile([P, BATCH, ROWS * W_BLOCKS], F32, name="xl_t")
-            first_row_of[j] = min((2 * SEG * j) // W_BLOCKS, WINDOW - ROWS)
-            xl_of[j] = xl_t
-
-        def project_mx(j, piece):
-            c, b = divmod(piece, BATCH)
-            window = b * X_ROWS + WINDOW_STEP * j
-            acc = psum_acc.tile([P, UNIT], F32, name="acc", tag="acc")
-            for d in range(4):
-                a = c * 4 + d
-                nc.tensor.matmul_mx(
-                    out=acc[:, d * WINDOW : (d + 1) * WINDOW],
-                    lhsT=w_codes[:, a * P : (a + 1) * P].bitcast(FP8X4),
-                    lhsT_scale=w_scales[:, a * P : (a + 1) * P],
-                    rhs=x_codes[:, window : window + WINDOW].bitcast(FP8X4),
-                    rhs_scale=x_scales[:, window : window + WINDOW],
-                    start=True,
-                    stop=True,
-                )
-            acc_of[piece] = acc
-
-        def project_bias(j, piece):
-            c, b = divmod(piece, BATCH)
-            first_row = first_row_of[j]
-            nc.vector.tensor_tensor(
-                out=xl_of[j][:, b, :].rearrange("p (r a) -> p r a", a=W_BLOCKS)[:, :, c * 4 : (c + 1) * 4],
-                in0=acc_of[piece][:].rearrange("p (d r) -> p r d", d=4)[:, first_row : first_row + ROWS, :],
-                in1=bias_t[:, c * 4 : (c + 1) * 4].unsqueeze(1).to_broadcast([P, ROWS, 4]),
-                op=ALU.add,
-            )
 
         def segments(j, unit):
             first = 2 * SEG * j - W_BLOCKS * first_row_of[j] + unit * UNIT
@@ -263,7 +285,8 @@ def tile_ka_attention_heads_mod_pa_kernel(tc, x, lin_w, lin_b, grid, coef, shift
         def whole_turns(i):
             jm = place(i)[0]
             whole = loop.tile([P, BATCH, UNIT], I32, name="whole", bufs=WHOLE_AHEAD + 1)
-            nc.gpsimd.tensor_scalar(
+            engine = nc.vector if i < VECTOR_TURNS else nc.gpsimd
+            engine.tensor_scalar(
                 out=whole[:],
                 in0=xl_of_half(i),
                 scalar1=turns[:, jm : jm + 1],
@@ -343,21 +366,16 @@ def tile_ka_attention_heads_mod_pa_kernel(tc, x, lin_w, lin_b, grid, coef, shift
                 return [i]
             return [i, i + 1, i + 2] if i % UNITS == 1 else []
 
-        first_row_of, xl_of, acc_of, x_nat_of, resident_of = {}, {}, {}, {}, {}
+        x_nat_of, resident_of = {}, {}
         whole_of, sine_of, coef_t_of, sums_of = {}, {}, {}, {}
         pieces = BATCH * GROUPS
-        group_tiles(0)
-        for piece in range(pieces + 1):
-            if piece < pieces:
-                project_mx(0, piece)
-            if piece >= 1:
-                project_bias(0, piece - 1)
         for part in range(PARTS_AHEAD):
             sort_coef(part)
-        for i in range(WHOLE_AHEAD):
-            whole_turns(i)
+        whole_turns(0)
         for i in range(halves + STORE_LAG + 1):
-            if i + WHOLE_AHEAD < halves:
+            if i + 1 < VECTOR_TURNS:
+                whole_turns(i + 1)
+            if VECTOR_TURNS <= i + WHOLE_AHEAD < halves:
                 whole_turns(i + WHOLE_AHEAD)
             if i - STORE_LAG in block_ended:
                 store(block_ended[i - STORE_LAG])
@@ -368,11 +386,6 @@ def tile_ka_attention_heads_mod_pa_kernel(tc, x, lin_w, lin_b, grid, coef, shift
                 sine(i - SINE_LAG)
             if 0 <= i - PRODUCT_LAG + 1 < halves:
                 turn_coef(i - PRODUCT_LAG + 1)
-            ending = i - SUM_LAG + SHIFT_AHEAD
-            if 0 <= ending < halves and ending % 4 == 1:
-                turn_shift(ending // 4)
-            if i - SUM_LAG in block_ended:
-                add_up(block_ended[i - SUM_LAG])
             j, local = divmod(i, halves_per_group)
             if j + 1 < GROUPS:
                 first_piece = 0 if j == 0 else 6
@@ -390,7 +403,13 @@ def tile_ka_attention_heads_mod_pa_kernel(tc, x, lin_w, lin_b, grid, coef, shift
                 lay_naturally(0, i - FIRST_RESIDENT + 4)
             if FIRST_RESIDENT - 2 <= i < FIRST_RESIDENT:
                 make_resident(0, i - FIRST_RESIDENT + 2)
+            ending = i - SUM_LAG + SHIFT_AHEAD
+            if 0 <= ending < halves and ending % 4 == 1:
+                turn_shift(ending // 4)
+            if i - SUM_LAG in block_ended:
+                add_up(block_ended[i - SUM_LAG])
             if 0 <= i - PRODUCT_LAG < halves:
                 four_terms(i - PRODUCT_LAG)
-            if PARTS_AHEAD + i < 2 * TILES:
-                sort_coef(PARTS_AHEAD + i)
+            part, odd = divmod(i, 2)
+            if not odd and PARTS_AHEAD + part < 2 * TILES:
+                sort_coef(PARTS_AHEAD + part)

import math
from contextlib import ExitStack

import concourse.mybir as mybir
from concourse.masks import make_identity

F32 = mybir.dt.float32
BF16 = mybir.dt.bfloat16
I32 = mybir.dt.int32
U32 = mybir.dt.uint32
U8 = mybir.dt.uint8
FP8X4 = mybir.dt.float8_e4m3fn_x4
ALU = mybir.AluOpType
ACT = mybir.ActivationFunctionType

P = 128
BATCH = 2
X_ROWS = 384
K = 512
W_BLOCKS = 20
GROUPS = 5
FREQS = 8
SEG = 128
TILES = 12
UNIT_TILES = 4
UNITS = TILES // UNIT_TILES
UNIT = UNIT_TILES * SEG
WINDOW = 128
WINDOW_STEP = 64
ROWS = 78
TERMS = 8
WHOLE_AHEAD = 3
SINE_LAG = 1
PRODUCT_LAG = 4
SUM_LAG = 5
STORE_LAG = 6
SHIFT_AHEAD = 2

PART = SEG // 2
PARTS_AHEAD = 6
WORDS = GROUPS * FREQS // 2
TILE_WORDS = SEG * WORDS

VECTOR_TURNS = 6
FIRST_RESIDENT = 6
SINE_BUFS = 10
SHIFT_PAIRS = 3

FLOPS = 2 * BATCH * X_ROWS * K * W_BLOCKS * P


def tile_ka_attention_heads_mod_pa_kernel(tc, x, lin_w, lin_b, grid, coef, shift, out):
    nc = tc.nc

    x_view = x.rearrange("b h p k -> (b h p) k").rearrange("(a p) k -> p a k", p=P)
    w_view = lin_w.rearrange("(a p) k -> p a k", p=P)
    coef_view = coef.rearrange("(t q d) m j -> t q (d m j)", q=P, d=SEG)
    shift_view = shift.rearrange("o h g p (c d) -> (p c) (o h g) d", d=SEG)
    out_view = out.rearrange("b h g p (c d) -> (p c) b (h g) d", d=SEG)

    with ExitStack() as stack:
        keep = stack.enter_context(tc.tile_pool(name="keep", bufs=1))
        psum_turn = stack.enter_context(tc.psum_pool(name="psum_turn", bufs=3))
        psum_acc = stack.enter_context(tc.psum_pool(name="psum_acc", bufs=2))
        psum_sums = stack.enter_context(tc.psum_pool(name="psum_sums", bufs=1))
        psum_xl = stack.enter_context(tc.psum_pool(name="psum_xl", bufs=BATCH))

        x_tiles = BATCH * X_ROWS // P
        x_codes = keep.tile([P, x_tiles * P], U32, name="x_codes", align_bytes=64)
        x_scales = keep.tile([P, x_tiles * P], U8, name="x_scales", align_bytes=64)
        w_codes = keep.tile([P, W_BLOCKS * P], U32, name="w_codes", align_bytes=64)
        w_scales = keep.tile([P, W_BLOCKS * P], U8, name="w_scales", align_bytes=64)
        coef_sb = keep.tile([P, (TILES + 1) * TILE_WORDS * 2], BF16, name="coef_sb")
        ident = keep.tile([P, P], F32, name="ident")
        ident_bf = keep.tile([P, P], BF16, name="ident_bf")
        bias_t = keep.tile([P, W_BLOCKS], F32, name="bias_t")
        turns = keep.tile([P, GROUPS * FREQS], F32, name="turns")

        def coef_place(t):
            return coef_sb[:, t * TILE_WORDS * 2 : (t + 1) * TILE_WORDS * 2]

        def sort_coef(part):
            t, s = divmod(part, 2)
            values = slice(s * PART, (s + 1) * PART)
            nc.scalar.copy(
                out=coef_place(t).bitcast(F32).rearrange("p (g r d) -> p g d r", r=4, d=SEG)[:, :, values, :],
                in_=coef_place(t + 1).bitcast(F32).rearrange("p (d g r) -> p g d r", r=4, d=SEG)[:, :, values, :],
            )
            sorted_parts.add(part)

        def is_laid_out(t):
            return 2 * min(t + 1, TILES - 1) in sorted_parts and 2 * t + 1 in sorted_parts

        sorted_parts = set()
        shift_of = {}

        def load_shift(pair):
            shift_of[pair] = keep.tile([P, 2, SEG], BF16, name="shift_sb", bufs=SHIFT_PAIRS)
            nc.sync.dma_start(out=shift_of[pair][:], in_=shift_view[:, 2 * pair : 2 * pair + 2, :])

        xl_pool = stack.enter_context(tc.tile_pool(name="xl", bufs=2))
        first_row_of, xl_of, acc_of = {}, {}, {}

        def group_tiles(j):
            xl_t = xl_pool.tile([P, BATCH, ROWS * W_BLOCKS], F32, name="xl_t")
            first_row_of[j] = min((2 * SEG * j) // W_BLOCKS, WINDOW - ROWS)
            xl_of[j] = xl_t

        def project_mx(j, piece):
            c, b = divmod(piece, BATCH)
            window = b * X_ROWS + WINDOW_STEP * j
            acc = psum_acc.tile([P, UNIT], F32, name="acc", tag="acc")
            for d in range(4):
                a = c * 4 + d
                nc.tensor.matmul_mx(
                    out=acc[:, d * WINDOW : (d + 1) * WINDOW],
                    lhsT=w_codes[:, a * P : (a + 1) * P].bitcast(FP8X4),
                    lhsT_scale=w_scales[:, a * P : (a + 1) * P],
                    rhs=x_codes[:, window : window + WINDOW].bitcast(FP8X4),
                    rhs_scale=x_scales[:, window : window + WINDOW],
                    start=True,
                    stop=True,
                )
            acc_of[piece] = acc

        def project_bias(j, piece):
            c, b = divmod(piece, BATCH)
            first_row = first_row_of[j]
            nc.vector.tensor_tensor(
                out=xl_of[j][:, b, :].rearrange("p (r a) -> p r a", a=W_BLOCKS)[:, :, c * 4 : (c + 1) * 4],
                in0=acc_of[piece][:].rearrange("p (d r) -> p r d", d=4)[:, first_row : first_row + ROWS, :],
                in1=bias_t[:, c * 4 : (c + 1) * 4].unsqueeze(1).to_broadcast([P, ROWS, 4]),
                op=ALU.add,
            )

        stack.enter_context(tc.manual_schedule())
        with tc.tile_pool(name="prep", bufs=1) as prep:
            x_raw = prep.tile([P, x_tiles * K], BF16, name="x_raw")
            w_raw = prep.tile([P, W_BLOCKS * K], BF16, name="w_raw")
            x_grouped = prep.tile([P, x_tiles * P * 4], BF16, name="x_grouped", align_bytes=64)
            w_grouped = prep.tile([P, W_BLOCKS * P * 4], BF16, name="w_grouped", align_bytes=64)
            bias_rows = prep.tile([P, P], BF16, name="bias_rows")
            bias_rows_f = prep.tile([P, P], F32, name="bias_rows_f")
            grid_row = prep.tile([P, GROUPS * FREQS], BF16, name="grid_row")
            ones = prep.tile([P, P], BF16, name="ones")

            nc.vector.memset(bias_rows[:], 0.0)
            nc.vector.memset(grid_row[:], 0.0)
            nc.vector.memset(ones[:], 1.0)
            make_identity(nc, ident[:])
            make_identity(nc, ident_bf[:])

            nc.scalar.dma_start(out=bias_rows[0:W_BLOCKS, :], in_=lin_b.rearrange("(a d) -> a d", d=P))
            nc.scalar.dma_start(out=grid_row[0:1, :], in_=grid.rearrange("(o j) m -> o (j m)", o=1))
            nc.sync.dma_start(out=x_raw[:].rearrange("p (a k) -> p a k", k=K), in_=x_view)
            for c in range(GROUPS):
                nc.sync.dma_start(
                    out=w_raw[:, c * 4 * K : (c + 1) * 4 * K].rearrange("p (a k) -> p a k", k=K),
                    in_=w_view[:, c * 4 : (c + 1) * 4, :],
                )

            for t in range(TILES):
                if t == UNIT_TILES:
                    for pair in range(SHIFT_PAIRS - 1):
                        load_shift(pair)
                nc.sync.dma_start(
                    out=coef_sb[:, (t + 1) * TILE_WORDS * 2 : (t + 2) * TILE_WORDS * 2], in_=coef_view[t]
                )

            def put_k_on_partitions(raw, grouped, pairs):
                words = raw[:].bitcast(F32)
                grouped_words = grouped[:].bitcast(F32)
                for pair in pairs:
                    bank = psum_turn.tile([P, UNIT], F32, name="turned", tag="bank")
                    for a in range(2):
                        for u in range(2):
                            first = (pair * 2 + a) * 2 * P
                            nc.tensor.transpose(
                                bank[:, (a * 2 + u) * P : (a * 2 + u + 1) * P],
                                words[:, first + u : first + 2 * P : 2],
                                ident[:],
                            )
                    dst = grouped_words[:, pair * UNIT : (pair + 1) * UNIT].rearrange(
                        "p (a r u) -> p a r u", a=2, u=2
                    )
                    src = bank[:].rearrange("p (a u r) -> p a r u", a=2, u=2)
                    nc.scalar.copy(out=dst, in_=src)

            def quantise(grouped, codes, scales, first, n):
                nc.vector.quantize_mx(
                    out=codes[:, first : first + n].bitcast(FP8X4),
                    scales=scales[:, first : first + n],
                    in_=grouped[:, first * 4 : (first + n) * 4],
                )

            put_k_on_partitions(x_raw, x_grouped, range(x_tiles // 2))
            group_tiles(0)
            for c in range(GROUPS + 3):
                if c < GROUPS:
                    put_k_on_partitions(w_raw, w_grouped, (2 * c, 2 * c + 1))
                if c == 0:
                    quantise(x_grouped, x_codes, x_scales, 0, 512)
                    quantise(x_grouped, x_codes, x_scales, 512, x_tiles * P - 512)
                elif c <= GROUPS:
                    quantise(w_grouped, w_codes, w_scales, (c - 1) * 512, 512)
                if c == 2:
                    nc.vector.tensor_copy(out=bias_rows_f[:], in_=bias_rows[:])
                    bias_ps = psum_turn.tile([P, UNIT], F32, name="bias_ps", tag="bank")
                    nc.tensor.transpose(bias_ps[:, 0:P], bias_rows_f[:], ident[:])
                    nc.vector.tensor_copy(out=bias_t[:], in_=bias_ps[:, 0:W_BLOCKS])
                for b in range(BATCH):
                    if c >= 3:
                        project_bias(0, (c - 3) * BATCH + b)
                for b in range(BATCH):
                    if 2 <= c < GROUPS + 2:
                        project_mx(0, (c - 2) * BATCH + b)

            grid_ps = psum_turn.tile([P, UNIT], F32, name="grid_ps", tag="bank")
            nc.tensor.matmul(
                out=grid_ps[:, 0 : GROUPS * FREQS], lhsT=ones[:], rhs=grid_row[:], start=True, stop=True
            )
            nc.vector.tensor_scalar(
                out=turns[:],
                in0=grid_ps[:, 0 : GROUPS * FREQS],
                scalar1=1.0 / (2.0 * math.pi),
                scalar2=None,
                op0=ALU.mult,
            )

        loop = stack.enter_context(tc.tile_pool(name="loop", bufs=2))
        halves = GROUPS * FREQS * UNITS
        halves_per_group = FREQS * UNITS

        def segments(j, unit):
            first = 2 * SEG * j - W_BLOCKS * first_row_of[j] + unit * UNIT
            return xl_of[j][:, :, first : first + UNIT]

        def new_sine():
            return loop.tile([P, BATCH, UNIT], F32, name="sine", bufs=SINE_BUFS)

        def lay_naturally(j, b):
            if b == 0:
                x_nat_of[j] = new_sine()
            bank = psum_turn.tile([P, UNIT], F32, name="turned", tag="bank")
            for t in range(UNIT_TILES):
                tile = slice(t * SEG, (t + 1) * SEG)
                nc.tensor.transpose(bank[:, tile], segments(j, 0)[:, b, tile], ident[:])
            nc.scalar.copy(out=x_nat_of[j][:, b, :], in_=bank[:])

        def make_resident(j, b):
            bank = psum_xl.tile([P, UNIT], F32, name="xl_ps")
            for t in range(UNIT_TILES):
                tile = slice(t * SEG, (t + 1) * SEG)
                nc.tensor.transpose(bank[:, tile], x_nat_of[j][:, b, tile], ident[:])
            resident_of[j, b] = bank

        order = [0, 1, 3, 4, 2, 5] + list(range(6, halves))
        block_ended = {}
        for block in range(halves // 2):
            block_ended[max(order.index(2 * block), order.index(2 * block + 1))] = block

        def place(i):
            jm, unit = divmod(order[i], UNITS)
            j, m = divmod(jm, FREQS)
            return jm, j, m, unit

        def turn_coef(i):
            jm, j, m, unit = place(i)
            column = m * GROUPS + j
            bank = psum_turn.tile([P, 2 * UNIT], BF16, name="coef_ps", tag="bank")
            for t in range(UNIT_TILES):
                tile = unit * UNIT_TILES + t
                if is_laid_out(tile):
                    values = coef_place(tile).rearrange("p (w d e) -> p w e d", w=WORDS, e=2)[:, column // 2, column % 2, :]
                else:
                    values = coef_place(tile + 1).rearrange("p (d c) -> p c d", d=SEG)[:, column, :]
                nc.tensor.transpose(bank[:, t * SEG : (t + 1) * SEG], values, ident_bf[:])
            coef_t_of[i] = bank[:, 0:UNIT]


        def xl_of_half(i):
            jm, j, m, unit = place(i)
            return segments(j, unit)

        def whole_turns(i):
            jm = place(i)[0]
            whole = loop.tile([P, BATCH, UNIT], I32, name="whole", bufs=WHOLE_AHEAD + 1)
            engine = nc.vector if i < VECTOR_TURNS else nc.gpsimd
            engine.tensor_scalar(
                out=whole[:],
                in0=xl_of_half(i),
                scalar1=turns[:, jm : jm + 1],
                scalar2=0.0,
                op0=ALU.mult,
                op1=ALU.add,
            )
            whole_of[i] = whole

        def rest_of_turn(i):
            jm, j, m, unit = place(i)
            sine_of[i] = new_sine()

            def subtract(where, xl):
                nc.vector.scalar_tensor_tensor(
                    out=sine_of[i][where],
                    in0=xl,
                    scalar=turns[:, jm : jm + 1],
                    in1=whole_of[i][where],
                    op0=ALU.mult,
                    op1=ALU.subtract,
                )

            if unit == 0 and i >= FIRST_RESIDENT:
                for b in range(BATCH):
                    subtract((slice(None), b, slice(None)), resident_of[j, b][:])
            else:
                subtract(slice(None), segments(j, unit))

        def sine(i):
            nc.scalar.activation(out=sine_of[i][:], in_=sine_of[i][:], func=ACT.Sin, scale=2.0 * math.pi)

        def four_terms(i):
            nc.vector.tensor_tensor(
                out=sine_of[i][:],
                in0=sine_of[i][:],
                in1=coef_t_of[i].unsqueeze(1).to_broadcast([P, BATCH, UNIT]),
                op=ALU.mult,
            )

        def add_up(block):
            sums = psum_sums.tile([P, 2 * BATCH, SEG], F32, name="sums")
            for b in range(BATCH):
                terms = [shift_t_of[block // 2][:, block % 2, :]]
                for e in range(TERMS):
                    products = sine_of[order.index(2 * block + e // UNIT_TILES)]
                    t = e % UNIT_TILES
                    terms.append(products[:, b, t * SEG : (t + 1) * SEG])
                for n, term in enumerate(terms):
                    nc.tensor.matmul(
                        out=sums[:, b, :],
                        lhsT=term,
                        rhs=ident[:],
                        is_transpose=True,
                        start=(n == 0),
                        stop=(n == TERMS),
                    )
            sums_of[block] = sums

        def turn_shift(pair):
            bank = psum_acc.tile([P, 2 * UNIT], BF16, name="shift_ps", tag="acc")
            for n in range(2):
                nc.tensor.transpose(bank[:, n * SEG : (n + 1) * SEG], shift_of[pair][:, n, :], ident_bf[:])
            if pair + SHIFT_PAIRS - 1 < halves // 4:
                load_shift(pair + SHIFT_PAIRS - 1)
            shift_t_of[pair] = loop.tile([P, 2, SEG], F32, name="shift_t", bufs=3)
            nc.scalar.copy(out=shift_t_of[pair][:], in_=bank[:, 0 : 2 * SEG].rearrange("p (n q) -> p n q", n=2))

        def store(block):
            total = loop.tile([P, BATCH, SEG], F32, name="total")
            nc.scalar.copy(out=total[:], in_=sums_of[block][:, 0:BATCH, :])
            nc.sync.dma_start(out=out_view[:, :, block, :], in_=total[:])

        shift_t_of = {}
        def subtracted_in_step(i):
            if i < FIRST_RESIDENT or i == FIRST_RESIDENT:
                return [i]
            return [i, i + 1, i + 2] if i % UNITS == 1 else []

        x_nat_of, resident_of = {}, {}
        whole_of, sine_of, coef_t_of, sums_of = {}, {}, {}, {}
        pieces = BATCH * GROUPS
        for part in range(PARTS_AHEAD):
            sort_coef(part)
        whole_turns(0)
        for i in range(halves + STORE_LAG + 1):
            if i + 1 < VECTOR_TURNS:
                whole_turns(i + 1)
            if VECTOR_TURNS <= i + WHOLE_AHEAD < halves:
                whole_turns(i + WHOLE_AHEAD)
            if i - STORE_LAG in block_ended:
                store(block_ended[i - STORE_LAG])
            for n in subtracted_in_step(i):
                if n < halves:
                    rest_of_turn(n)
            if 0 <= i - SINE_LAG < halves:
                sine(i - SINE_LAG)
            if 0 <= i - PRODUCT_LAG + 1 < halves:
                turn_coef(i - PRODUCT_LAG + 1)
            j, local = divmod(i, halves_per_group)
            if j + 1 < GROUPS:
                first_piece = 0 if j == 0 else 6
                if local == first_piece:
                    group_tiles(j + 1)
                if first_piece < local <= first_piece + pieces:
                    project_bias(j + 1, local - first_piece - 1)
                if first_piece <= local < first_piece + pieces:
                    project_mx(j + 1, local - first_piece)
                if 17 <= local < 17 + BATCH:
                    lay_naturally(j + 1, local - 17)
                if 20 <= local < 20 + BATCH:
                    make_resident(j + 1, local - 20)
            if FIRST_RESIDENT - 4 <= i < FIRST_RESIDENT - 2:
                lay_naturally(0, i - FIRST_RESIDENT + 4)
            if FIRST_RESIDENT - 2 <= i < FIRST_RESIDENT:
                make_resident(0, i - FIRST_RESIDENT + 2)
            ending = i - SUM_LAG + SHIFT_AHEAD
            if 0 <= ending < halves and ending % 4 == 1:
                turn_shift(ending // 4)
            if i - SUM_LAG in block_ended:
                add_up(block_ended[i - SUM_LAG])
            if 0 <= i - PRODUCT_LAG < halves:
                four_terms(i - PRODUCT_LAG)
            part, odd = divmod(i, 2)
            if not odd and PARTS_AHEAD + part < 2 * TILES:
                sort_coef(PARTS_AHEAD + part)
